import numpy as np
import ml_dtypes


def mxq(x, axis, fmt="e4m3"):
    dtype, down = {"e4m3": (ml_dtypes.float8_e4m3fn, 7), "e5m2": (ml_dtypes.float8_e5m2, 14)}[fmt]
    v = np.moveaxis(np.asarray(x, np.float32).astype(ml_dtypes.bfloat16).astype(np.float64), axis, -1)
    blocks = v.reshape(v.shape[:-1] + (-1, 32))
    amax = np.abs(blocks).max(-1, keepdims=True)
    byte = np.maximum(np.where(amax > 0, np.frexp(amax)[1] - 1 + 127, 0) - down, 1)
    scale = np.exp2(byte - 127.0)
    codes = (blocks / scale).astype(np.float32).astype(dtype).astype(np.float64)
    return np.moveaxis((codes * scale).reshape(v.shape), -1, axis)


WIDE = False


def mx_kscale(k):
    if not WIDE:
        return np.ones(k)
    levels = np.array([10, -10, 5, -5, 0])
    a = np.random.permutation(np.resize(levels, k // 512 * 4)).reshape(k // 512, 4)
    idx = np.arange(k)
    return np.exp2(a[idx // 512, idx % 128 // 32])


BF16 = ml_dtypes.bfloat16


def bf(x):
    return np.asarray(x, np.float32).astype(BF16)


def f64(x):
    return np.asarray(x).astype(np.float64)


B, H, L, D, DV = 2, 8, 512, 128, 256


def setup_inputs():
    keep = (np.random.random((B, L, L)) < 0.75) | np.eye(L, dtype=bool)
    s = mx_kscale(L)
    q = np.random.standard_normal((B, H, L, D)) * 1.2
    k = np.random.standard_normal((B, H, L, D)) * 1.2
    v = np.random.standard_normal((B, H, L, DV))
    pe_q = np.random.standard_normal((B, H, L, D)) * 1.2
    pe_k = np.random.standard_normal((B, H, L, D)) * 1.2
    pe_q[..., 0] = 1.0
    pe_k[..., 0] += np.log(s) * np.sqrt(D)
    v = v / s[:, None] * s.mean()
    return {"q": bf(q), "k": bf(k), "v": bf(v), "pe_q": bf(pe_q), "pe_k": bf(pe_k), "mask": bf(keep)}


def reference(q, k, v, pe_q, pe_k, mask):
    scale = D ** (-0.5)
    attn = (f64(q) @ f64(k).transpose(0, 1, 3, 2) + f64(pe_q) @ f64(pe_k).transpose(0, 1, 3, 2)) * scale
    attn = np.where(f64(mask)[:, None, :, :] != 0.0, attn, -np.inf)
    e = np.exp(attn - attn.max(-1, keepdims=True))
    return (mxq(e, 3, "e4m3") @ mxq(f64(v), 2, "e4m3")) / e.sum(-1, keepdims=True)

@@ -1,0 +1,305 @@
+from contextlib import ExitStack
+
+import concourse.mybir as mybir
+from concourse.masks import make_identity
+
+F32 = mybir.dt.float32
+BF16 = mybir.dt.bfloat16
+U32 = mybir.dt.uint32
+U8 = mybir.dt.uint8
+FP8X4 = mybir.dt.float8_e4m3fn_x4
+ALU = mybir.AluOpType
+ACT = mybir.ActivationFunctionType
+AX = mybir.AxisListType
+
+B, H, L, D, DV = 2, 8, 512, 128, 256
+P = 128
+NH = B * H
+NSTEP = 2 * NH
+SCALE = D ** (-0.5)
+BIG = 1.0e30
+FLOPS = NH * (2 * 2 * L * L * D + 2 * L * L * DV)
+
+
+def tile_attention_t_kernel(tc, q, k, v, pe_q, pe_k, mask, out):
+    nc = tc.nc
+    with ExitStack() as ctx:
+        const = ctx.enter_context(tc.tile_pool(name="const", bufs=1))
+        raw = ctx.enter_context(tc.tile_pool(name="raw", bufs=4))
+        tsb = ctx.enter_context(tc.tile_pool(name="tsb", bufs=3))
+        work = ctx.enter_context(tc.tile_pool(name="work", bufs=3))
+        small = ctx.enter_context(tc.tile_pool(name="small", bufs=5))
+        outp = ctx.enter_context(tc.tile_pool(name="outp", bufs=3))
+        ps_a = ctx.enter_context(tc.psum_pool(name="ps_a", bufs=1))
+        ps_s = ctx.enter_context(tc.psum_pool(name="ps_s", bufs=3))
+        ps_c = ctx.enter_context(tc.psum_pool(name="ps_c", bufs=2))
+        ps_d = ctx.enter_context(tc.psum_pool(name="ps_d", bufs=2))
+        ctx.enter_context(tc.manual_schedule())
+
+        qq, kk, vr, q_t, k_t, tps = {}, {}, {}, {}, {}, {}
+        sps, tt, mn, ee, rsum, rs = {}, {}, {}, {}, {}, {}
+        e_t, xx, gq, ecodes, escl = {}, {}, {}, {}, {}
+        vg, vcodes, vscl, ops, osb = {}, {}, {}, {}, {}
+
+        def rows4(ap):
+            return ap.rearrange("(a l) c -> a l c", l=4)
+
+        def load(h):
+            b, hh = divmod(h, H)
+            kk[h] = raw.tile([P, 4, 2 * D], BF16, name="kk")
+            qq[h] = raw.tile([P, 4, 2 * D], BF16, name="qq")
+            vr[h] = raw.tile([P, 4, DV], BF16, name="vr")
+            nc.sync.dma_start(out=kk[h][:, :, 0:D], in_=rows4(k[b, hh]))
+            nc.sync.dma_start(out=kk[h][:, :, D : 2 * D], in_=rows4(pe_k[b, hh]))
+            nc.sync.dma_start(out=qq[h][:, :, 0:D], in_=rows4(q[b, hh]))
+            nc.sync.dma_start(out=qq[h][:, :, D : 2 * D], in_=rows4(pe_q[b, hh]))
+
+        def load_v(h):
+            b, hh = divmod(h, H)
+            nc.sync.dma_start(out=vr[h][:], in_=rows4(v[b, hh]))
+
+        def side_head(n):
+            return (n + 3) // 2 if n % 2 == 1 else (n + 2) // 2
+
+        def a_side(n):
+            h = side_head(n)
+            if not 0 <= h < NH:
+                return
+            src = kk[h] if n % 2 == 1 else qq[h]
+            src32 = src[:].rearrange("p l c -> p (l c)").bitcast(F32)
+            tps[n] = ps_a.tile([P, 4, P], F32, name="tps")
+            for l in range(4):
+                nc.tensor.transpose(tps[n][:, l, :], src32[:, l * P : (l + 1) * P], ident_f[:])
+
+        def evac_a(n):
+            h = side_head(n)
+            if not 0 <= h < NH:
+                return
+            if n % 2 == 1:
+                k_t[h] = tsb.tile([P, L], F32, name="k_t")
+                dst = k_t[h]
+            else:
+                q_t[h] = tsb.tile([P, L], F32, name="q_t")
+                dst = q_t[h]
+            nc.scalar.copy(out=dst[:], in_=tps[n][:].rearrange("p l a -> p (l a)"))
+
+        def scores(n, jj):
+            if not 0 <= n < NSTEP:
+                return
+            h = n // 2
+            j = 2 * (n % 2) + jj
+            qb = q_t[h][:].bitcast(BF16).rearrange("p (c e) -> p c e", e=2)
+            kb = k_t[h][:].bitcast(BF16).rearrange("p (c e) -> p c e", e=2)
+            sps[(n, jj)] = ps_s.tile([P, L], F32, name="sps")
+            for e in range(2):
+                nc.tensor.matmul(
+                    sps[(n, jj)][:],
+                    lhsT=qb[:, j * P : (j + 1) * P, e],
+                    rhs=kb[:, :, e],
+                    start=(e == 0),
+                    stop=(e == 1),
+                )
+
+        def stt(n, jj):
+            if not 0 <= n < NSTEP:
+                return
+            b = n // (2 * H)
+            j = 2 * (n % 2) + jj
+            if jj == 0:
+                tt[n] = work.tile([P, 2, L], F32, name="tt")
+            nc.vector.scalar_tensor_tensor(
+                out=tt[n][:, jj, :],
+                in0=sps[(n, jj)][:],
+                scalar=-SCALE,
+                in1=capn[b][:, j, :],
+                op0=ALU.mult,
+                op1=ALU.max,
+            )
+
+        def reduce_min(n):
+            if not 0 <= n < NSTEP:
+                return
+            mn[n] = small.tile([P, 2], F32, name="mn")
+            nc.vector.tensor_reduce(out=mn[n][:], in_=tt[n][:], axis=AX.X, op=ALU.min)
+
+        def exp(n, jj):
+            if not 0 <= n < NSTEP:
+                return
+            if jj == 0:
+                ee[n] = work.tile([P, 2, L], BF16, name="ee")
+                rsum[n] = small.tile([P, 2], F32, name="rsum")
+            nc.scalar.activation(
+                out=ee[n][:, jj, :],
+                in_=tt[n][:, jj, :],
+                func=ACT.Exp,
+                bias=mn[n][:, jj : jj + 1],
+                scale=-1.0,
+                accum_out=rsum[n][:, jj : jj + 1],
+            )
+
+        def e_transposes(n, jj):
+            if not 0 <= n < NSTEP:
+                return
+            if jj == 0:
+                e_t[n] = ps_c.tile([P, 2, 4, P], BF16, name="e_t")
+            for t in range(4):
+                nc.tensor.transpose(e_t[n][:, jj, t, :], ee[n][:, jj, t * P : (t + 1) * P], ident_b[:])
+
+        def evac_c(n):
+            if not 0 <= n < NSTEP:
+                return
+            xx[n] = work.tile([P, 2, 4, P], BF16, name="xx")
+            nc.scalar.copy(
+                out=xx[n][:].rearrange("p j t q -> p (j t q)"),
+                in_=e_t[n][:].rearrange("p j t q -> p (j t q)"),
+            )
+
+        def regroup_e(n):
+            if not 0 <= n < NSTEP:
+                return
+            gq[n] = work.tile([P, 2, P, 4], BF16, name="gq", align_bytes=64)
+            nc.gpsimd.tensor_scalar(
+                out=gq[n][:],
+                in0=xx[n][:].rearrange("p j t q -> p j q t"),
+                scalar1=1.0,
+                scalar2=0.0,
+                op0=ALU.mult,
+                op1=ALU.add,
+            )
+
+        def quant_e(n):
+            if not 0 <= n < NSTEP:
+                return
+            ecodes[n] = work.tile([P, 2 * P], U32, name="ecodes", align_bytes=64)
+            escl[n] = work.tile([P, 2 * P], U8, name="escl", align_bytes=64)
+            nc.vector.quantize_mx(
+                out=ecodes[n][:].bitcast(FP8X4),
+                scales=escl[n][:],
+                in_=gq[n][:].rearrange("p j q t -> p (j q t)"),
+            )
+
+        def regroup_v(n):
+            if not 0 <= n < NSTEP:
+                return
+            h, half = n // 2, n % 2
+            if half == 0:
+                vg[h] = work.tile([P, DV, 4], BF16, name="vg", align_bytes=64)
+            cols = slice(half * P, (half + 1) * P)
+            nc.gpsimd.tensor_scalar(
+                out=vg[h][:, cols, :],
+                in0=vr[h][:, :, cols].rearrange("p t c -> p c t"),
+                scalar1=1.0,
+                scalar2=0.0,
+                op0=ALU.mult,
+                op1=ALU.add,
+            )
+
+        def quant_v(h):
+            if not 0 <= h < NH:
+                return
+            vcodes[h] = work.tile([P, DV], U32, name="vcodes", align_bytes=64)
+            vscl[h] = work.tile([P, DV], U8, name="vscl", align_bytes=64)
+            nc.vector.quantize_mx(
+                out=vcodes[h][:].bitcast(FP8X4),
+                scales=vscl[h][:],
+                in_=vg[h][:].rearrange("p c t -> p (c t)"),
+            )
+
+        def mx(n, jj):
+            if not 0 <= n < NSTEP:
+                return
+            h = n // 2
+            if jj == 0:
+                ops[n] = ps_d.tile([P, 2, DV], F32, name="ops")
+            cols = slice(jj * P, (jj + 1) * P)
+            nc.tensor.matmul_mx(
+                out=ops[n][:, jj, :],
+                lhsT=ecodes[n][:, cols].bitcast(FP8X4),
+                lhsT_scale=escl[n][:, cols],
+                rhs=vcodes[h][:].bitcast(FP8X4),
+                rhs_scale=vscl[h][:],
+                start=True,
+                stop=True,
+            )
+
+        def recip(n):
+            if not 0 <= n < NSTEP:
+                return
+            rs[n] = small.tile([P, 2], F32, name="rs")
+            nc.vector.reciprocal(out=rs[n][:], in_=rsum[n][:])
+
+        def evac_d(n, jj):
+            if not 0 <= n < NSTEP:
+                return
+            h = n // 2
+            j = 2 * (n % 2) + jj
+            if j == 0:
+                osb[h] = outp.tile([P, 4, DV], F32, name="osb")
+            nc.scalar.activation(
+                out=osb[h][:, j, :],
+                in_=ops[n][:, jj, :],
+                func=ACT.Copy,
+                scale=rs[n][:, jj : jj + 1],
+            )
+
+        def store(n):
+            if not 0 <= n < NSTEP or n % 2 == 0:
+                return
+            h = n // 2
+            b, hh = divmod(h, H)
+            nc.sync.dma_start(out=rows4(out[b, hh]), in_=osb[h][:])
+
+        def cap_views(b, l):
+            dst = capn[b][:, l, :].rearrange("p (t a) -> p t a", t=4)
+            src = m_raw[b][:, l, :].rearrange("p (a t) -> p t a", t=4)
+            return dst, src
+
+        ident_f = const.tile([P, P], F32, name="ident_f")
+        ident_b = const.tile([P, P], BF16, name="ident_b")
+        make_identity(nc, ident_f[:])
+        make_identity(nc, ident_b[:])
+        m_raw = [const.tile([P, 4, L], BF16, name="m_raw%d" % b) for b in range(B)]
+        capn = [const.tile([P, 4, L], BF16, name="capn%d" % b) for b in range(B)]
+
+        load(0)
+        nc.sync.dma_start(out=m_raw[0][:], in_=rows4(mask[0]))
+        load_v(0)
+        load(1)
+        load_v(1)
+        load(2)
+        load_v(2)
+        nc.sync.dma_start(out=m_raw[1][:], in_=rows4(mask[1]))
+        for l in range(4):
+            dst, src = cap_views(0, l)
+            nc.vector.tensor_scalar(out=dst, in0=src, scalar1=-0.5, scalar2=-2.0 * BIG, op0=ALU.add, op1=ALU.mult)
+
+        for n in range(-3, NSTEP + 4):
+            if n >= 0 and n % 2 == 0 and n // 2 + 3 < NH:
+                load(n // 2 + 3)
+                load_v(n // 2 + 3)
+            a_side(n)
+            stt(n, 0)
+            scores(n + 1, 0)
+            mx(n - 3, 0)
+            mx(n - 3, 1)
+            stt(n, 1)
+            scores(n + 1, 1)
+            exp(n - 1, 0)
+            exp(n - 1, 1)
+            e_transposes(n - 1, 0)
+            e_transposes(n - 1, 1)
+            reduce_min(n)
+            evac_a(n)
+            evac_d(n - 3, 0)
+            evac_d(n - 3, 1)
+            store(n - 3)
+            evac_c(n - 1)
+            regroup_e(n - 2)
+            regroup_v(n)
+            if 2 <= n < 6:
+                dst, src = cap_views(1, n - 2)
+                nc.gpsimd.tensor_scalar(out=dst, in0=src, scalar1=-0.5, scalar2=-2.0 * BIG, op0=ALU.add, op1=ALU.mult)
+            quant_e(n - 2)
+            if n % 2 == 0:
+                quant_v(n // 2 - 1)
+            recip(n - 1)

@@ -10,7 +10,6 @@ U8 = mybir.dt.uint8
 FP8X4 = mybir.dt.float8_e4m3fn_x4
 ALU = mybir.AluOpType
 ACT = mybir.ActivationFunctionType
-AX = mybir.AxisListType
 
 B, H, L, D, DV = 2, 8, 512, 128, 256
 P = 128
@@ -20,6 +19,11 @@ SCALE = D ** (-0.5)
 BIG = 1.0e30
 FLOPS = NH * (2 * 2 * L * L * D + 2 * L * L * DV)
 
+LAG_TS, LAG_EXP, LAG_T, LAG_EVC, LAG_QE, LAG_MX, LAG_EVD, LAG_RC = 1, 2, 3, 4, 5, 6, 7, 3
+TAIL_C = 4
+TAIL_D = 5
+MASK1_AT = 6
+
 
 def tile_attention_t_kernel(tc, q, k, v, pe_q, pe_k, mask, out):
     nc = tc.nc
@@ -27,19 +31,24 @@ def tile_attention_t_kernel(tc, q, k, v, pe_q, pe_k, mask, out):
         const = ctx.enter_context(tc.tile_pool(name="const", bufs=1))
         raw = ctx.enter_context(tc.tile_pool(name="raw", bufs=4))
         tsb = ctx.enter_context(tc.tile_pool(name="tsb", bufs=3))
-        work = ctx.enter_context(tc.tile_pool(name="work", bufs=3))
-        small = ctx.enter_context(tc.tile_pool(name="small", bufs=5))
-        outp = ctx.enter_context(tc.tile_pool(name="outp", bufs=3))
+        tts = ctx.enter_context(tc.tile_pool(name="tts", bufs=6))
+        work = ctx.enter_context(tc.tile_pool(name="work", bufs=4))
+        small = ctx.enter_context(tc.tile_pool(name="small", bufs=12))
+        vgp = ctx.enter_context(tc.tile_pool(name="vgp", bufs=1))
+        outp = ctx.enter_context(tc.tile_pool(name="outp", bufs=4))
+        ps_s = ctx.enter_context(tc.psum_pool(name="ps_s", bufs=4))
         ps_a = ctx.enter_context(tc.psum_pool(name="ps_a", bufs=1))
-        ps_s = ctx.enter_context(tc.psum_pool(name="ps_s", bufs=3))
         ps_c = ctx.enter_context(tc.psum_pool(name="ps_c", bufs=2))
-        ps_d = ctx.enter_context(tc.psum_pool(name="ps_d", bufs=2))
+        ps_d = ctx.enter_context(tc.psum_pool(name="ps_d", bufs=1))
         ctx.enter_context(tc.manual_schedule())
 
         qq, kk, vr, q_t, k_t, tps = {}, {}, {}, {}, {}, {}
         sps, tt, mn, ee, rsum, rs = {}, {}, {}, {}, {}, {}
-        e_t, xx, gq, ecodes, escl = {}, {}, {}, {}, {}
-        vg, vcodes, vscl, ops, osb = {}, {}, {}, {}, {}
+        e_t, gq, ecodes, escl = {}, {}, {}, {}
+        vg, vcodes, vscl, ops, osb, m_t = {}, {}, {}, {}, {}, {}
+
+        def live(d):
+            return 0 <= d < NSTEP
 
         def rows4(ap):
             return ap.rearrange("(a l) c -> a l c", l=4)
@@ -51,143 +60,146 @@ def tile_attention_t_kernel(tc, q, k, v, pe_q, pe_k, mask, out):
             vr[h] = raw.tile([P, 4, DV], BF16, name="vr")
             nc.sync.dma_start(out=kk[h][:, :, 0:D], in_=rows4(k[b, hh]))
             nc.sync.dma_start(out=kk[h][:, :, D : 2 * D], in_=rows4(pe_k[b, hh]))
+            if h == 0:
+                nc.sync.dma_start(out=m_raw[0][:, 0:2, :], in_=rows4(mask[0])[:, 0:2, :])
             nc.sync.dma_start(out=qq[h][:, :, 0:D], in_=rows4(q[b, hh]))
             nc.sync.dma_start(out=qq[h][:, :, D : 2 * D], in_=rows4(pe_q[b, hh]))
+            if h == 0:
+                nc.sync.dma_start(out=m_raw[0][:, 2:4, :], in_=rows4(mask[0])[:, 2:4, :])
 
         def load_v(h):
             b, hh = divmod(h, H)
             nc.sync.dma_start(out=vr[h][:], in_=rows4(v[b, hh]))
 
-        def side_head(n):
-            return (n + 3) // 2 if n % 2 == 1 else (n + 2) // 2
+        def side(i):
+            return (i % 2 == 0), (i + 2) // 2 if i % 2 == 0 else (i + 1) // 2
 
-        def a_side(n):
-            h = side_head(n)
+        def a_transposes(i, blocks):
+            is_k, h = side(i)
             if not 0 <= h < NH:
                 return
-            src = kk[h] if n % 2 == 1 else qq[h]
+            src = kk[h] if is_k else qq[h]
             src32 = src[:].rearrange("p l c -> p (l c)").bitcast(F32)
-            tps[n] = ps_a.tile([P, 4, P], F32, name="tps")
-            for l in range(4):
-                nc.tensor.transpose(tps[n][:, l, :], src32[:, l * P : (l + 1) * P], ident_f[:])
+            if blocks[0] == 0:
+                tps[i] = ps_a.tile([P, 4, P], F32, name="tps")
+            for l in blocks:
+                nc.tensor.transpose(tps[i][:, l, :], src32[:, l * P : (l + 1) * P], ident_f[:])
 
-        def evac_a(n):
-            h = side_head(n)
+        def evac_a(i):
+            is_k, h = side(i)
             if not 0 <= h < NH:
                 return
-            if n % 2 == 1:
+            if is_k:
                 k_t[h] = tsb.tile([P, L], F32, name="k_t")
                 dst = k_t[h]
             else:
                 q_t[h] = tsb.tile([P, L], F32, name="q_t")
                 dst = q_t[h]
-            nc.scalar.copy(out=dst[:], in_=tps[n][:].rearrange("p l a -> p (l a)"))
+            src = tps[i][:].rearrange("p l a -> p (l a)")
+            if i < 2 or is_k:
+                nc.scalar.copy(out=dst[:], in_=src)
+            else:
+                nc.vector.tensor_copy(out=dst[:], in_=src)
 
-        def scores(n, jj):
-            if not 0 <= n < NSTEP:
+        def score_mm(d, jj, e):
+            if not live(d):
                 return
-            h = n // 2
-            j = 2 * (n % 2) + jj
+            h = d // 2
+            j = 2 * (d % 2) + jj
             qb = q_t[h][:].bitcast(BF16).rearrange("p (c e) -> p c e", e=2)
             kb = k_t[h][:].bitcast(BF16).rearrange("p (c e) -> p c e", e=2)
-            sps[(n, jj)] = ps_s.tile([P, L], F32, name="sps")
-            for e in range(2):
+            if e == 0:
+                sps[(d, jj)] = ps_s.tile([P, L], F32, name="sps")
+            nc.tensor.matmul(
+                sps[(d, jj)][:],
+                lhsT=qb[:, j * P : (j + 1) * P, e],
+                rhs=kb[:, :, e],
+                start=(e == 0),
+                stop=False,
+            )
+
+        def score_mask(d, jj, blocks):
+            if not live(d):
+                return
+            b = d // (2 * H)
+            j = 2 * (d % 2) + jj
+            for t in blocks:
                 nc.tensor.matmul(
-                    sps[(n, jj)][:],
-                    lhsT=qb[:, j * P : (j + 1) * P, e],
-                    rhs=kb[:, :, e],
-                    start=(e == 0),
-                    stop=(e == 1),
+                    sps[(d, jj)][:, t * P : (t + 1) * P],
+                    lhsT=cap_t[b][:, j, t, :],
+                    rhs=ident_f[:],
+                    is_transpose=True,
+                    start=False,
+                    stop=(t == 3),
                 )
 
-        def stt(n, jj):
-            if not 0 <= n < NSTEP:
+        def scale_min(d, jj):
+            if not live(d):
                 return
-            b = n // (2 * H)
-            j = 2 * (n % 2) + jj
-            if jj == 0:
-                tt[n] = work.tile([P, 2, L], F32, name="tt")
-            nc.vector.scalar_tensor_tensor(
-                out=tt[n][:, jj, :],
-                in0=sps[(n, jj)][:],
-                scalar=-SCALE,
-                in1=capn[b][:, j, :],
+            tt[(d, jj)] = tts.tile([P, L], F32, name="tt")
+            mn[(d, jj)] = small.tile([P, 1], F32, name="mn")
+            nc.vector.tensor_scalar(
+                out=tt[(d, jj)][:],
+                in0=sps[(d, jj)][:],
+                scalar1=-SCALE,
+                scalar2=None,
                 op0=ALU.mult,
-                op1=ALU.max,
+                op1=ALU.min,
+                accum_out=mn[(d, jj)][:],
             )
 
-        def reduce_min(n):
-            if not 0 <= n < NSTEP:
-                return
-            mn[n] = small.tile([P, 2], F32, name="mn")
-            nc.vector.tensor_reduce(out=mn[n][:], in_=tt[n][:], axis=AX.X, op=ALU.min)
-
-        def exp(n, jj):
-            if not 0 <= n < NSTEP:
+        def exp(d, jj):
+            if not live(d):
                 return
             if jj == 0:
-                ee[n] = work.tile([P, 2, L], BF16, name="ee")
-                rsum[n] = small.tile([P, 2], F32, name="rsum")
+                ee[d] = work.tile([P, 2, L], BF16, name="ee")
+                rsum[d] = small.tile([P, 2], F32, name="rsum")
             nc.scalar.activation(
-                out=ee[n][:, jj, :],
-                in_=tt[n][:, jj, :],
+                out=ee[d][:, jj, :],
+                in_=tt[(d, jj)][:],
                 func=ACT.Exp,
-                bias=mn[n][:, jj : jj + 1],
+                bias=mn[(d, jj)][:],
                 scale=-1.0,
-                accum_out=rsum[n][:, jj : jj + 1],
+                accum_out=rsum[d][:, jj : jj + 1],
             )
 
-        def e_transposes(n, jj):
-            if not 0 <= n < NSTEP:
+        def e_transposes(d, jj):
+            if not live(d):
                 return
             if jj == 0:
-                e_t[n] = ps_c.tile([P, 2, 4, P], BF16, name="e_t")
+                e_t[d] = ps_c.tile([P, 2, 4, P], BF16, name="e_t")
             for t in range(4):
-                nc.tensor.transpose(e_t[n][:, jj, t, :], ee[n][:, jj, t * P : (t + 1) * P], ident_b[:])
+                nc.tensor.transpose(e_t[d][:, jj, t, :], ee[d][:, jj, t * P : (t + 1) * P], ident_b[:])
 
-        def evac_c(n):
-            if not 0 <= n < NSTEP:
+        def evac_c(d, jj):
+            if not live(d):
                 return
-            xx[n] = work.tile([P, 2, 4, P], BF16, name="xx")
-            nc.scalar.copy(
-                out=xx[n][:].rearrange("p j t q -> p (j t q)"),
-                in_=e_t[n][:].rearrange("p j t q -> p (j t q)"),
-            )
+            if jj == 0:
+                gq[d] = work.tile([P, 2, P, 4], BF16, name="gq", align_bytes=64)
+            src = e_t[d][:, jj, :, :].rearrange("p t q -> p q t")
+            if d >= NSTEP - TAIL_C and d % 2 == 1:
+                nc.vector.tensor_copy(out=gq[d][:, jj, :, :], in_=src)
+            else:
+                nc.scalar.copy(out=gq[d][:, jj, :, :], in_=src)
 
-        def regroup_e(n):
-            if not 0 <= n < NSTEP:
+        def quant_e(d):
+            if not live(d):
                 return
-            gq[n] = work.tile([P, 2, P, 4], BF16, name="gq", align_bytes=64)
-            nc.gpsimd.tensor_scalar(
-                out=gq[n][:],
-                in0=xx[n][:].rearrange("p j t q -> p j q t"),
-                scalar1=1.0,
-                scalar2=0.0,
-                op0=ALU.mult,
-                op1=ALU.add,
-            )
-
-        def quant_e(n):
-            if not 0 <= n < NSTEP:
-                return
-            ecodes[n] = work.tile([P, 2 * P], U32, name="ecodes", align_bytes=64)
-            escl[n] = work.tile([P, 2 * P], U8, name="escl", align_bytes=64)
+            ecodes[d] = work.tile([P, 2 * P], U32, name="ecodes", align_bytes=64)
+            escl[d] = work.tile([P, 2 * P], U8, name="escl", align_bytes=64)
             nc.vector.quantize_mx(
-                out=ecodes[n][:].bitcast(FP8X4),
-                scales=escl[n][:],
-                in_=gq[n][:].rearrange("p j q t -> p (j q t)"),
+                out=ecodes[d][:].bitcast(FP8X4),
+                scales=escl[d][:],
+                in_=gq[d][:].rearrange("p j q t -> p (j q t)"),
             )
 
-        def regroup_v(n):
-            if not 0 <= n < NSTEP:
+        def regroup_v(h):
+            if not 0 <= h < NH:
                 return
-            h, half = n // 2, n % 2
-            if half == 0:
-                vg[h] = work.tile([P, DV, 4], BF16, name="vg", align_bytes=64)
-            cols = slice(half * P, (half + 1) * P)
+            vg[h] = vgp.tile([P, DV, 4], BF16, name="vg", align_bytes=64)
             nc.gpsimd.tensor_scalar(
-                out=vg[h][:, cols, :],
-                in0=vr[h][:, :, cols].rearrange("p t c -> p c t"),
+                out=vg[h][:],
+                in0=vr[h][:].rearrange("p t c -> p c t"),
                 scalar1=1.0,
                 scalar2=0.0,
                 op0=ALU.mult,
@@ -205,101 +217,132 @@ def tile_attention_t_kernel(tc, q, k, v, pe_q, pe_k, mask, out):
                 in_=vg[h][:].rearrange("p c t -> p (c t)"),
             )
 
-        def mx(n, jj):
-            if not 0 <= n < NSTEP:
+        def mx(d, jj):
+            if not live(d):
                 return
-            h = n // 2
+            h = d // 2
             if jj == 0:
-                ops[n] = ps_d.tile([P, 2, DV], F32, name="ops")
+                if d >= NSTEP - TAIL_D:
+                    ops[d] = ps_s.tile([P, 2, DV], F32, name="ops_tail", tag="sps")
+                else:
+                    ops[d] = ps_d.tile([P, 2, DV], F32, name="ops")
             cols = slice(jj * P, (jj + 1) * P)
             nc.tensor.matmul_mx(
-                out=ops[n][:, jj, :],
-                lhsT=ecodes[n][:, cols].bitcast(FP8X4),
-                lhsT_scale=escl[n][:, cols],
+                out=ops[d][:, jj, :],
+                lhsT=ecodes[d][:, cols].bitcast(FP8X4),
+                lhsT_scale=escl[d][:, cols],
                 rhs=vcodes[h][:].bitcast(FP8X4),
                 rhs_scale=vscl[h][:],
                 start=True,
                 stop=True,
             )
 
-        def recip(n):
-            if not 0 <= n < NSTEP:
+        def recip(d):
+            if not live(d):
                 return
-            rs[n] = small.tile([P, 2], F32, name="rs")
-            nc.vector.reciprocal(out=rs[n][:], in_=rsum[n][:])
+            rs[d] = small.tile([P, 2], F32, name="rs")
+            nc.vector.reciprocal(out=rs[d][:], in_=rsum[d][:])
 
-        def evac_d(n, jj):
-            if not 0 <= n < NSTEP:
+        def evac_d(d):
+            if not live(d):
                 return
-            h = n // 2
-            j = 2 * (n % 2) + jj
-            if j == 0:
-                osb[h] = outp.tile([P, 4, DV], F32, name="osb")
-            nc.scalar.activation(
-                out=osb[h][:, j, :],
-                in_=ops[n][:, jj, :],
-                func=ACT.Copy,
-                scale=rs[n][:, jj : jj + 1],
-            )
+            osb[d] = outp.tile([P, 2, DV], F32, name="osb")
+            if d >= NSTEP - TAIL_D:
+                for jj in range(2):
+                    nc.scalar.activation(
+                        out=osb[d][:, jj, :], in_=ops[d][:, jj, :], func=ACT.Copy, scale=rs[d][:, jj : jj + 1]
+                    )
+            else:
+                nc.vector.tensor_tensor(
+                    out=osb[d][:],
+                    in0=ops[d][:],
+                    in1=rs[d][:].unsqueeze(2).to_broadcast([P, 2, DV]),
+                    op=ALU.mult,
+                )
+            b, hh = divmod(d // 2, H)
+            j0 = 2 * (d % 2)
+            nc.sync.dma_start(out=rows4(out[b, hh])[:, j0 : j0 + 2, :], in_=osb[d][:])
 
-        def store(n):
-            if not 0 <= n < NSTEP or n % 2 == 0:
-                return
-            h = n // 2
-            b, hh = divmod(h, H)
-            nc.sync.dma_start(out=rows4(out[b, hh]), in_=osb[h][:])
+        def mask_transposes(b, j):
+            m_t[(b, j)] = ps_s.tile([P, 4, P], BF16, name="m_t", tag="sps")
+            src = m_raw[b][:, j, :].rearrange("p (a t) -> p t a", t=4)
+            for t in range(4):
+                nc.tensor.transpose(m_t[(b, j)][:, t, :], src[:, t, :], ident_b[:])
 
-        def cap_views(b, l):
-            dst = capn[b][:, l, :].rearrange("p (t a) -> p t a", t=4)
-            src = m_raw[b][:, l, :].rearrange("p (a t) -> p t a", t=4)
-            return dst, src
+        def cap_build(b, j, on_scalar):
+            dst = cap_t[b][:, j, :, :].rearrange("p t q -> p (t q)")
+            src = m_t[(b, j)][:].rearrange("p t q -> p (t q)")
+            if on_scalar:
+                nc.scalar.activation(out=dst, in_=src, func=ACT.Copy, bias=-BIG, scale=BIG)
+            else:
+                nc.vector.tensor_scalar(out=dst, in0=src, scalar1=-1.0, scalar2=BIG, op0=ALU.add, op1=ALU.mult)
 
         ident_f = const.tile([P, P], F32, name="ident_f")
         ident_b = const.tile([P, P], BF16, name="ident_b")
         make_identity(nc, ident_f[:])
         make_identity(nc, ident_b[:])
         m_raw = [const.tile([P, 4, L], BF16, name="m_raw%d" % b) for b in range(B)]
-        capn = [const.tile([P, 4, L], BF16, name="capn%d" % b) for b in range(B)]
+        cap_t = [const.tile([P, 4, 4, P], F32, name="cap_t%d" % b) for b in range(B)]
 
         load(0)
-        nc.sync.dma_start(out=m_raw[0][:], in_=rows4(mask[0]))
-        load_v(0)
         load(1)
+        load_v(0)
         load_v(1)
         load(2)
         load_v(2)
         nc.sync.dma_start(out=m_raw[1][:], in_=rows4(mask[1]))
-        for l in range(4):
-            dst, src = cap_views(0, l)
-            nc.vector.tensor_scalar(out=dst, in0=src, scalar1=-0.5, scalar2=-2.0 * BIG, op0=ALU.add, op1=ALU.mult)
+        regroup_v(0)
 
-        for n in range(-3, NSTEP + 4):
+        for n in range(-2, NSTEP + LAG_EVD + 1):
             if n >= 0 and n % 2 == 0 and n // 2 + 3 < NH:
                 load(n // 2 + 3)
                 load_v(n // 2 + 3)
-            a_side(n)
-            stt(n, 0)
-            scores(n + 1, 0)
-            mx(n - 3, 0)
-            mx(n - 3, 1)
-            stt(n, 1)
-            scores(n + 1, 1)
-            exp(n - 1, 0)
-            exp(n - 1, 1)
-            e_transposes(n - 1, 0)
-            e_transposes(n - 1, 1)
-            reduce_min(n)
+            scale_min(n - LAG_TS, 0)
+            scale_min(n - LAG_TS, 1)
+            exp(n - LAG_EXP, 0)
+            exp(n - LAG_EXP, 1)
+            if MASK1_AT <= n < MASK1_AT + 4:
+                mask_transposes(1, n - MASK1_AT)
+            if n >= 2:
+                score_mm(n, 0, 0)
+                a_transposes(n, [0, 1])
+                score_mm(n, 0, 1)
+                a_transposes(n, [2, 3])
+                score_mm(n, 1, 0)
+                score_mask(n, 0, [0, 1])
+                score_mm(n, 1, 1)
+                score_mask(n, 0, [2, 3])
+                score_mask(n, 1, [0, 1, 2, 3])
+            else:
+                score_mm(n, 0, 0)
+                score_mm(n, 0, 1)
+                score_mask(n, 0, [0, 1, 2, 3])
+                score_mm(n, 1, 0)
+                score_mm(n, 1, 1)
+                score_mask(n, 1, [0, 1, 2, 3])
+                if n == 0:
+                    mask_transposes(0, 2)
+                    mask_transposes(0, 3)
+                    cap_build(0, 2, True)
+                    cap_build(0, 3, True)
+                a_transposes(n, [0, 1, 2, 3])
+                if n == -2:
+                    mask_transposes(0, 0)
+                    mask_transposes(0, 1)
+                    cap_build(0, 0, False)
+                    cap_build(0, 1, False)
             evac_a(n)
-            evac_d(n - 3, 0)
-            evac_d(n - 3, 1)
-            store(n - 3)
-            evac_c(n - 1)
-            regroup_e(n - 2)
-            regroup_v(n)
-            if 2 <= n < 6:
-                dst, src = cap_views(1, n - 2)
-                nc.gpsimd.tensor_scalar(out=dst, in0=src, scalar1=-0.5, scalar2=-2.0 * BIG, op0=ALU.add, op1=ALU.mult)
-            quant_e(n - 2)
-            if n % 2 == 0:
+            e_transposes(n - LAG_T, 0)
+            e_transposes(n - LAG_T, 1)
+            evac_c(n - LAG_EVC, 0)
+            evac_c(n - LAG_EVC, 1)
+            evac_d(n - LAG_EVD)
+            if MASK1_AT <= n < MASK1_AT + 4:
+                cap_build(1, n - MASK1_AT, n % 2 == 0)
+            recip(n - LAG_RC)
+            quant_e(n - LAG_QE)
+            if n >= 2 and n % 2 == 0:
                 quant_v(n // 2 - 1)
-            recip(n - 1)
+                regroup_v(n // 2)
+            mx(n - LAG_MX, 0)
+            mx(n - LAG_MX, 1)

@@ -95,11 +95,15 @@ def tile_attention_t_kernel(tc, q, k, v, pe_q, pe_k, mask, out):
             else:
                 q_t[h] = tsb.tile([P, L], F32, name="q_t")
                 dst = q_t[h]
-            src = tps[i][:].rearrange("p l a -> p (l a)")
-            if i < 2 or is_k:
-                nc.scalar.copy(out=dst[:], in_=src)
+            if is_k:
+                nc.scalar.copy(
+                    out=dst[:].rearrange("p (u a e) -> p u a e", u=2, e=2),
+                    in_=tps[i][:].rearrange("p (u e) a -> p u a e", e=2),
+                )
+            elif i < 2:
+                nc.scalar.copy(out=dst[:], in_=tps[i][:].rearrange("p l a -> p (l a)"))
             else:
-                nc.vector.tensor_copy(out=dst[:], in_=src)
+                nc.vector.tensor_copy(out=dst[:], in_=tps[i][:].rearrange("p l a -> p (l a)"))
 
         def score_mm(d, jj, e):
             if not live(d):
@@ -167,20 +171,23 @@ def tile_attention_t_kernel(tc, q, k, v, pe_q, pe_k, mask, out):
             if not live(d):
                 return
             if jj == 0:
-                e_t[d] = ps_c.tile([P, 2, 4, P], BF16, name="e_t")
-            for t in range(4):
-                nc.tensor.transpose(e_t[d][:, jj, t, :], ee[d][:, jj, t * P : (t + 1) * P], ident_b[:])
+                e_t[d] = ps_c.tile([P, 2, 2, P], F32, name="e_t")
+            words = ee[d][:].rearrange("p j c -> p (j c)").bitcast(F32)
+            for u in range(2):
+                w0 = (2 * jj + u) * P
+                nc.tensor.transpose(e_t[d][:, jj, u, :], words[:, w0 : w0 + P], ident_f[:])
 
         def evac_c(d, jj):
             if not live(d):
                 return
             if jj == 0:
                 gq[d] = work.tile([P, 2, P, 4], BF16, name="gq", align_bytes=64)
-            src = e_t[d][:, jj, :, :].rearrange("p t q -> p q t")
+            src = e_t[d][:, jj, :, :].rearrange("p u q -> p q u")
+            dst = gq[d][:].rearrange("p j q t -> p (j q t)").bitcast(F32).rearrange("p (j q u) -> p j q u", j=2, u=2)[:, jj, :, :]
             if d >= NSTEP - TAIL_C and d % 2 == 1:
-                nc.vector.tensor_copy(out=gq[d][:, jj, :, :], in_=src)
+                nc.vector.tensor_copy(out=dst, in_=src)
             else:
-                nc.scalar.copy(out=gq[d][:, jj, :, :], in_=src)
+                nc.scalar.copy(out=dst, in_=src)
 
         def quant_e(d):
             if not live(d):
@@ -265,9 +272,14 @@ def tile_attention_t_kernel(tc, q, k, v, pe_q, pe_k, mask, out):
 
         def mask_transposes(b, j):
             m_t[(b, j)] = ps_s.tile([P, 4, P], BF16, name="m_t", tag="sps")
-            src = m_raw[b][:, j, :].rearrange("p (a t) -> p t a", t=4)
             for t in range(4):
-                nc.tensor.transpose(m_t[(b, j)][:, t, :], src[:, t, :], ident_b[:])
+                nc.tensor.transpose(m_t[(b, j)][:, t, :], m_perm[b][:, j, t * P : (t + 1) * P], ident_b[:])
+
+        def mask_permute(b, j0, j1):
+            nc.vector.tensor_copy(
+                out=m_perm[b][:, j0:j1, :].bitcast(F32).rearrange("p j (u a) -> p j u a", u=2),
+                in_=m_raw[b][:, j0:j1, :].bitcast(F32).rearrange("p j (a u) -> p j u a", u=2),
+            )
 
         def cap_build(b, j, on_scalar):
             dst = cap_t[b][:, j, :, :].rearrange("p t q -> p (t q)")
@@ -282,6 +294,7 @@ def tile_attention_t_kernel(tc, q, k, v, pe_q, pe_k, mask, out):
         make_identity(nc, ident_f[:])
         make_identity(nc, ident_b[:])
         m_raw = [const.tile([P, 4, L], BF16, name="m_raw%d" % b) for b in range(B)]
+        m_perm = [const.tile([P, 4, L], BF16, name="m_perm%d" % b) for b in range(B)]
         cap_t = [const.tile([P, 4, 4, P], F32, name="cap_t%d" % b) for b in range(B)]
 
         load(0)
@@ -292,6 +305,7 @@ def tile_attention_t_kernel(tc, q, k, v, pe_q, pe_k, mask, out):
         load_v(2)
         nc.sync.dma_start(out=m_raw[1][:], in_=rows4(mask[1]))
         regroup_v(0)
+        mask_permute(0, 0, 2)
 
         for n in range(-2, NSTEP + LAG_EVD + 1):
             if n >= 0 and n % 2 == 0 and n // 2 + 3 < NH:
@@ -301,6 +315,8 @@ def tile_attention_t_kernel(tc, q, k, v, pe_q, pe_k, mask, out):
             scale_min(n - LAG_TS, 1)
             exp(n - LAG_EXP, 0)
             exp(n - LAG_EXP, 1)
+            if n == MASK1_AT - 1:
+                mask_permute(1, 0, 4)
             if MASK1_AT <= n < MASK1_AT + 4:
                 mask_transposes(1, n - MASK1_AT)
             if n >= 2:
@@ -331,6 +347,7 @@ def tile_attention_t_kernel(tc, q, k, v, pe_q, pe_k, mask, out):
                     mask_transposes(0, 1)
                     cap_build(0, 0, False)
                     cap_build(0, 1, False)
+                    mask_permute(0, 2, 4)
             evac_a(n)
             e_transposes(n - LAG_T, 0)
             e_transposes(n - LAG_T, 1)

@@ -19,7 +19,7 @@ SCALE = D ** (-0.5)
 BIG = 1.0e30
 FLOPS = NH * (2 * 2 * L * L * D + 2 * L * L * DV)
 
-LAG_TS, LAG_EXP, LAG_T, LAG_EVC, LAG_QE, LAG_MX, LAG_EVD, LAG_RC = 1, 2, 3, 4, 5, 6, 7, 3
+LAG_TS, LAG_EXP, LAG_T, LAG_EVC, LAG_QE, LAG_MX, LAG_EVD, LAG_RC = 1, 2, 3, 4, 5, 6, 6, 3
 TAIL_C = 4
 TAIL_D = 5
 MASK1_AT = 6
@@ -325,9 +325,10 @@ def tile_attention_t_kernel(tc, q, k, v, pe_q, pe_k, mask, out):
                 score_mm(n, 0, 1)
                 a_transposes(n, [2, 3])
                 score_mm(n, 1, 0)
-                score_mask(n, 0, [0, 1])
+                mx(n - LAG_MX, 0)
+                mx(n - LAG_MX, 1)
                 score_mm(n, 1, 1)
-                score_mask(n, 0, [2, 3])
+                score_mask(n, 0, [0, 1, 2, 3])
                 score_mask(n, 1, [0, 1, 2, 3])
             else:
                 score_mm(n, 0, 0)
@@ -353,7 +354,6 @@ def tile_attention_t_kernel(tc, q, k, v, pe_q, pe_k, mask, out):
             e_transposes(n - LAG_T, 1)
             evac_c(n - LAG_EVC, 0)
             evac_c(n - LAG_EVC, 1)
-            evac_d(n - LAG_EVD)
             if MASK1_AT <= n < MASK1_AT + 4:
                 cap_build(1, n - MASK1_AT, n % 2 == 0)
             recip(n - LAG_RC)
@@ -361,5 +361,4 @@ def tile_attention_t_kernel(tc, q, k, v, pe_q, pe_k, mask, out):
             if n >= 2 and n % 2 == 0:
                 quant_v(n // 2 - 1)
                 regroup_v(n // 2)
-            mx(n - LAG_MX, 0)
-            mx(n - LAG_MX, 1)
+            evac_d(n - LAG_EVD)

@@ -100,10 +100,8 @@ def tile_attention_t_kernel(tc, q, k, v, pe_q, pe_k, mask, out):
                     out=dst[:].rearrange("p (u a e) -> p u a e", u=2, e=2),
                     in_=tps[i][:].rearrange("p (u e) a -> p u a e", e=2),
                 )
-            elif i < 2:
-                nc.scalar.copy(out=dst[:], in_=tps[i][:].rearrange("p l a -> p (l a)"))
             else:
-                nc.vector.tensor_copy(out=dst[:], in_=tps[i][:].rearrange("p l a -> p (l a)"))
+                nc.scalar.copy(out=dst[:], in_=tps[i][:].rearrange("p l a -> p (l a)"))
 
         def score_mm(d, jj, e):
             if not live(d):

@@ -19,7 +19,7 @@ SCALE = D ** (-0.5)
 BIG = 1.0e30
 FLOPS = NH * (2 * 2 * L * L * D + 2 * L * L * DV)
 
-LAG_TS, LAG_EXP, LAG_T, LAG_EVC, LAG_QE, LAG_MX, LAG_EVD, LAG_RC = 1, 2, 3, 4, 5, 6, 6, 3
+LAG_TS, LAG_EXP, LAG_T, LAG_EVC, LAG_QE, LAG_MX, LAG_EVD, LAG_RC = 1, 2, 2, 3, 4, 5, 5, 3
 TAIL_C = 4
 TAIL_D = 5
 MASK1_AT = 6
@@ -57,43 +57,50 @@ def tile_attention_t_kernel(tc, q, k, v, pe_q, pe_k, mask, out):
             b, hh = divmod(h, H)
             kk[h] = raw.tile([P, 4, 2 * D], BF16, name="kk")
             qq[h] = raw.tile([P, 4, 2 * D], BF16, name="qq")
-            vr[h] = raw.tile([P, 4, DV], BF16, name="vr")
             nc.sync.dma_start(out=kk[h][:, :, 0:D], in_=rows4(k[b, hh]))
             nc.sync.dma_start(out=kk[h][:, :, D : 2 * D], in_=rows4(pe_k[b, hh]))
             if h == 0:
-                nc.sync.dma_start(out=m_raw[0][:, 0:2, :], in_=rows4(mask[0])[:, 0:2, :])
-            nc.sync.dma_start(out=qq[h][:, :, 0:D], in_=rows4(q[b, hh]))
-            nc.sync.dma_start(out=qq[h][:, :, D : 2 * D], in_=rows4(pe_q[b, hh]))
-            if h == 0:
-                nc.sync.dma_start(out=m_raw[0][:, 2:4, :], in_=rows4(mask[0])[:, 2:4, :])
+                for l0 in (0, 2):
+                    nc.sync.dma_start(out=qq[h][:, l0 : l0 + 2, 0:D], in_=rows4(q[b, hh])[:, l0 : l0 + 2, :])
+                    nc.sync.dma_start(out=qq[h][:, l0 : l0 + 2, D : 2 * D], in_=rows4(pe_q[b, hh])[:, l0 : l0 + 2, :])
+                    nc.sync.dma_start(out=m_raw[0][:, l0 : l0 + 2, :], in_=rows4(mask[0])[:, l0 : l0 + 2, :])
+            else:
+                nc.sync.dma_start(out=qq[h][:, :, 0:D], in_=rows4(q[b, hh]))
+                nc.sync.dma_start(out=qq[h][:, :, D : 2 * D], in_=rows4(pe_q[b, hh]))
 
         def load_v(h):
             b, hh = divmod(h, H)
+            vr[h] = raw.tile([P, 4, DV], BF16, name="vr")
             nc.sync.dma_start(out=vr[h][:], in_=rows4(v[b, hh]))
 
         def side(i):
             return (i % 2 == 0), (i + 2) // 2 if i % 2 == 0 else (i + 1) // 2
 
-        def a_transposes(i, blocks):
+        def a_transposes(i, blocks, borrowed=False):
             is_k, h = side(i)
             if not 0 <= h < NH:
                 return
             src = kk[h] if is_k else qq[h]
             src32 = src[:].rearrange("p l c -> p (l c)").bitcast(F32)
             if blocks[0] == 0:
-                tps[i] = ps_a.tile([P, 4, P], F32, name="tps")
+                if borrowed:
+                    tps[i] = ps_c.tile([P, 4, P], F32, name="tps_start", tag="e_t")
+                else:
+                    tps[i] = ps_a.tile([P, 4, P], F32, name="tps")
             for l in blocks:
                 nc.tensor.transpose(tps[i][:, l, :], src32[:, l * P : (l + 1) * P], ident_f[:])
 
-        def evac_a(i):
+        def evac_a(i, l0=0, l1=4):
             is_k, h = side(i)
             if not 0 <= h < NH:
                 return
             if is_k:
                 k_t[h] = tsb.tile([P, L], F32, name="k_t")
                 dst = k_t[h]
-            else:
+            elif l0 == 0:
                 q_t[h] = tsb.tile([P, L], F32, name="q_t")
+                dst = q_t[h]
+            else:
                 dst = q_t[h]
             if is_k:
                 nc.scalar.copy(
@@ -101,7 +108,7 @@ def tile_attention_t_kernel(tc, q, k, v, pe_q, pe_k, mask, out):
                     in_=tps[i][:].rearrange("p (u e) a -> p u a e", e=2),
                 )
             else:
-                nc.scalar.copy(out=dst[:], in_=tps[i][:].rearrange("p l a -> p (l a)"))
+                nc.scalar.copy(out=dst[:, l0 * P : l1 * P], in_=tps[i][:, l0:l1, :].rearrange("p l a -> p (l a)"))
 
         def score_mm(d, jj, e):
             if not live(d):
@@ -155,14 +162,15 @@ def tile_attention_t_kernel(tc, q, k, v, pe_q, pe_k, mask, out):
                 return
             if jj == 0:
                 ee[d] = work.tile([P, 2, L], BF16, name="ee")
-                rsum[d] = small.tile([P, 2], F32, name="rsum")
+                if d % 2 == 0:
+                    rsum[d // 2] = small.tile([P, 4], F32, name="rsum")
             nc.scalar.activation(
                 out=ee[d][:, jj, :],
                 in_=tt[(d, jj)][:],
                 func=ACT.Exp,
                 bias=mn[(d, jj)][:],
                 scale=-1.0,
-                accum_out=rsum[d][:, jj : jj + 1],
+                accum_out=rsum[d // 2][:, 2 * (d % 2) + jj : 2 * (d % 2) + jj + 1],
             )
 
         def e_transposes(d, jj):
@@ -175,13 +183,12 @@ def tile_attention_t_kernel(tc, q, k, v, pe_q, pe_k, mask, out):
                 w0 = (2 * jj + u) * P
                 nc.tensor.transpose(e_t[d][:, jj, u, :], words[:, w0 : w0 + P], ident_f[:])
 
-        def evac_c(d, jj):
+        def evac_c(d):
             if not live(d):
                 return
-            if jj == 0:
-                gq[d] = work.tile([P, 2, P, 4], BF16, name="gq", align_bytes=64)
-            src = e_t[d][:, jj, :, :].rearrange("p u q -> p q u")
-            dst = gq[d][:].rearrange("p j q t -> p (j q t)").bitcast(F32).rearrange("p (j q u) -> p j q u", j=2, u=2)[:, jj, :, :]
+            gq[d] = work.tile([P, 2, P, 4], BF16, name="gq", align_bytes=64)
+            src = e_t[d][:].rearrange("p j u q -> p j q u")
+            dst = gq[d][:].rearrange("p j q t -> p (j q t)").bitcast(F32).rearrange("p (j q u) -> p j q u", j=2, u=2)
             if d >= NSTEP - TAIL_C and d % 2 == 1:
                 nc.vector.tensor_copy(out=dst, in_=src)
             else:
@@ -243,25 +250,26 @@ def tile_attention_t_kernel(tc, q, k, v, pe_q, pe_k, mask, out):
             )
 
         def recip(d):
-            if not live(d):
+            if not live(d) or d % 2 == 0:
                 return
-            rs[d] = small.tile([P, 2], F32, name="rs")
-            nc.vector.reciprocal(out=rs[d][:], in_=rsum[d][:])
+            rs[d // 2] = small.tile([P, 4], F32, name="rs")
+            nc.vector.reciprocal(out=rs[d // 2][:], in_=rsum[d // 2][:])
 
         def evac_d(d):
             if not live(d):
                 return
             osb[d] = outp.tile([P, 2, DV], F32, name="osb")
+            r0 = 2 * (d % 2)
             if d >= NSTEP - TAIL_D:
                 for jj in range(2):
                     nc.scalar.activation(
-                        out=osb[d][:, jj, :], in_=ops[d][:, jj, :], func=ACT.Copy, scale=rs[d][:, jj : jj + 1]
+                        out=osb[d][:, jj, :], in_=ops[d][:, jj, :], func=ACT.Copy, scale=rs[d // 2][:, r0 + jj : r0 + jj + 1]
                     )
             else:
                 nc.vector.tensor_tensor(
                     out=osb[d][:],
                     in0=ops[d][:],
-                    in1=rs[d][:].unsqueeze(2).to_broadcast([P, 2, DV]),
+                    in1=rs[d // 2][:, r0 : r0 + 2].unsqueeze(2).to_broadcast([P, 2, DV]),
                     op=ALU.mult,
                 )
             b, hh = divmod(d // 2, H)
@@ -298,65 +306,79 @@ def tile_attention_t_kernel(tc, q, k, v, pe_q, pe_k, mask, out):
         load(0)
         load(1)
         load_v(0)
-        load_v(1)
         load(2)
-        load_v(2)
+        load_v(1)
+        load(3)
         nc.sync.dma_start(out=m_raw[1][:], in_=rows4(mask[1]))
+        load_v(2)
         regroup_v(0)
         mask_permute(0, 0, 2)
 
-        for n in range(-2, NSTEP + LAG_EVD + 1):
-            if n >= 0 and n % 2 == 0 and n // 2 + 3 < NH:
+        a_transposes(-2, [0, 1, 2, 3])
+        evac_a(-2)
+        a_transposes(-1, [0, 1], borrowed=True)
+        evac_a(-1, 0, 2)
+        mask_transposes(0, 0)
+        mask_transposes(0, 1)
+        cap_build(0, 0, False)
+        cap_build(0, 1, False)
+        for jj in range(2):
+            score_mm(0, jj, 0)
+            score_mm(0, jj, 1)
+            score_mask(0, jj, [0, 1, 2, 3])
+        scale_min(0, 0)
+        mask_permute(0, 2, 4)
+        exp(0, 0)
+        a_transposes(-1, [2, 3], borrowed=True)
+        evac_a(-1, 2, 4)
+        a_transposes(0, [0, 1, 2, 3], borrowed=True)
+        evac_a(0)
+        mask_transposes(0, 2)
+        mask_transposes(0, 3)
+        scale_min(0, 1)
+        cap_build(0, 2, False)
+        cap_build(0, 3, False)
+        exp(0, 1)
+        a_transposes(1, [0, 1, 2, 3])
+        evac_a(1)
+        for jj in range(2):
+            score_mm(1, jj, 0)
+            score_mm(1, jj, 1)
+            score_mask(1, jj, [0, 1, 2, 3])
+
+        for n in range(2, NSTEP + LAG_EVD + 1):
+            if n % 2 == 0 and n // 2 + 3 < NH:
                 load(n // 2 + 3)
-                load_v(n // 2 + 3)
+            if n % 2 == 0 and n // 2 + 2 < NH:
+                load_v(n // 2 + 2)
             scale_min(n - LAG_TS, 0)
             scale_min(n - LAG_TS, 1)
-            exp(n - LAG_EXP, 0)
-            exp(n - LAG_EXP, 1)
+            if n - LAG_EXP >= 1:
+                exp(n - LAG_EXP, 0)
+                exp(n - LAG_EXP, 1)
             if n == MASK1_AT - 1:
                 mask_permute(1, 0, 4)
             if MASK1_AT <= n < MASK1_AT + 4:
                 mask_transposes(1, n - MASK1_AT)
-            if n >= 2:
-                score_mm(n, 0, 0)
-                a_transposes(n, [0, 1])
-                score_mm(n, 0, 1)
-                a_transposes(n, [2, 3])
-                score_mm(n, 1, 0)
-                mx(n - LAG_MX, 0)
-                mx(n - LAG_MX, 1)
-                score_mm(n, 1, 1)
-                score_mask(n, 0, [0, 1, 2, 3])
-                score_mask(n, 1, [0, 1, 2, 3])
-            else:
-                score_mm(n, 0, 0)
-                score_mm(n, 0, 1)
-                score_mask(n, 0, [0, 1, 2, 3])
-                score_mm(n, 1, 0)
-                score_mm(n, 1, 1)
-                score_mask(n, 1, [0, 1, 2, 3])
-                if n == 0:
-                    mask_transposes(0, 2)
-                    mask_transposes(0, 3)
-                    cap_build(0, 2, True)
-                    cap_build(0, 3, True)
-                a_transposes(n, [0, 1, 2, 3])
-                if n == -2:
-                    mask_transposes(0, 0)
-                    mask_transposes(0, 1)
-                    cap_build(0, 0, False)
-                    cap_build(0, 1, False)
-                    mask_permute(0, 2, 4)
+            score_mm(n, 0, 0)
+            a_transposes(n, [0, 1])
+            score_mm(n, 0, 1)
+            a_transposes(n, [2, 3])
+            score_mm(n, 1, 0)
+            mx(n - LAG_MX, 0)
+            mx(n - LAG_MX, 1)
+            score_mm(n, 1, 1)
+            score_mask(n, 0, [0, 1, 2, 3])
+            score_mask(n, 1, [0, 1, 2, 3])
             evac_a(n)
             e_transposes(n - LAG_T, 0)
             e_transposes(n - LAG_T, 1)
-            evac_c(n - LAG_EVC, 0)
-            evac_c(n - LAG_EVC, 1)
+            evac_c(n - LAG_EVC)
             if MASK1_AT <= n < MASK1_AT + 4:
                 cap_build(1, n - MASK1_AT, n % 2 == 0)
             recip(n - LAG_RC)
             quant_e(n - LAG_QE)
-            if n >= 2 and n % 2 == 0:
+            if n % 2 == 0:
                 quant_v(n // 2 - 1)
                 regroup_v(n // 2)
             evac_d(n - LAG_EVD)

@@ -15,6 +15,7 @@ B, H, L, D, DV = 2, 8, 512, 128, 256
 P = 128
 NH = B * H
 NSTEP = 2 * NH
+N_WARM = 7
 SCALE = D ** (-0.5)
 BIG = 1.0e30
 FLOPS = NH * (2 * 2 * L * L * D + 2 * L * L * DV)
@@ -302,6 +303,12 @@ def tile_attention_t_kernel(tc, q, k, v, pe_q, pe_k, mask, out):
         m_raw = [const.tile([P, 4, L], BF16, name="m_raw%d" % b) for b in range(B)]
         m_perm = [const.tile([P, 4, L], BF16, name="m_perm%d" % b) for b in range(B)]
         cap_t = [const.tile([P, 4, 4, P], F32, name="cap_t%d" % b) for b in range(B)]
+
+        warm = const.tile([P, 2 * P], BF16, name="warm")
+        warm_ps = ps_s.tile([P, 2 * P], F32, name="warm_ps", tag="sps")
+        nc.vector.memset(warm[:], 0.0)
+        for i in range(N_WARM):
+            nc.tensor.matmul(warm_ps[:], lhsT=warm[:, 0:P], rhs=warm[:], start=True, stop=True)
 
         load(0)
         load(1)

@@ -16,6 +16,7 @@ P = 128
 NH = B * H
 NSTEP = 2 * NH
 N_WARM = 7
+E_COLS = 2 * P * 4
 SCALE = D ** (-0.5)
 BIG = 1.0e30
 FLOPS = NH * (2 * 2 * L * L * D + 2 * L * L * DV)
@@ -35,7 +36,7 @@ def tile_attention_t_kernel(tc, q, k, v, pe_q, pe_k, mask, out):
         tts = ctx.enter_context(tc.tile_pool(name="tts", bufs=6))
         work = ctx.enter_context(tc.tile_pool(name="work", bufs=4))
         small = ctx.enter_context(tc.tile_pool(name="small", bufs=12))
-        vgp = ctx.enter_context(tc.tile_pool(name="vgp", bufs=1))
+        evp = ctx.enter_context(tc.tile_pool(name="evp", bufs=2))
         outp = ctx.enter_context(tc.tile_pool(name="outp", bufs=4))
         ps_s = ctx.enter_context(tc.psum_pool(name="ps_s", bufs=4))
         ps_a = ctx.enter_context(tc.psum_pool(name="ps_a", bufs=1))
@@ -46,7 +47,7 @@ def tile_attention_t_kernel(tc, q, k, v, pe_q, pe_k, mask, out):
         qq, kk, vr, q_t, k_t, tps = {}, {}, {}, {}, {}, {}
         sps, tt, mn, ee, rsum, rs = {}, {}, {}, {}, {}, {}
         e_t, gq, ecodes, escl = {}, {}, {}, {}
-        vg, vcodes, vscl, ops, osb, m_t = {}, {}, {}, {}, {}, {}
+        vcodes, vscl, ops, osb, m_t = {}, {}, {}, {}, {}
 
         def live(d):
             return 0 <= d < NSTEP
@@ -187,47 +188,48 @@ def tile_attention_t_kernel(tc, q, k, v, pe_q, pe_k, mask, out):
         def evac_c(d):
             if not live(d):
                 return
-            gq[d] = work.tile([P, 2, P, 4], BF16, name="gq", align_bytes=64)
+            if d % 2 == 1 or d == NSTEP - 2:
+                gq[d] = work.tile([P, E_COLS], BF16, name="gq", align_bytes=64)
             src = e_t[d][:].rearrange("p j u q -> p j q u")
-            dst = gq[d][:].rearrange("p j q t -> p (j q t)").bitcast(F32).rearrange("p (j q u) -> p j q u", j=2, u=2)
+            dst = gq[d][:, 0:E_COLS].bitcast(F32).rearrange("p (j q u) -> p j q u", j=2, u=2)
             if d >= NSTEP - TAIL_C and d % 2 == 1:
                 nc.vector.tensor_copy(out=dst, in_=src)
             else:
                 nc.scalar.copy(out=dst, in_=src)
 
+        def quantize(values, width):
+            codes = work.tile([P, width], U32, name="codes%d" % width, align_bytes=64)
+            scales = work.tile([P, width], U8, name="scales%d" % width, align_bytes=64)
+            nc.vector.quantize_mx(out=codes[:].bitcast(FP8X4), scales=scales[:], in_=values)
+            return codes, scales
+
+        def quant_last_v():
+            codes, scales = quantize(v_last[:], DV)
+            vcodes[NH - 1], vscl[NH - 1] = codes[:], scales[:]
+
         def quant_e(d):
             if not live(d):
                 return
-            ecodes[d] = work.tile([P, 2 * P], U32, name="ecodes", align_bytes=64)
-            escl[d] = work.tile([P, 2 * P], U8, name="escl", align_bytes=64)
-            nc.vector.quantize_mx(
-                out=ecodes[d][:].bitcast(FP8X4),
-                scales=escl[d][:],
-                in_=gq[d][:].rearrange("p j q t -> p (j q t)"),
-            )
+            with_v = d % 2 == 0 and d < NSTEP - 2
+            ecodes[d], escl[d] = quantize(gq[d][:], 2 * P + (DV if with_v else 0))
+            if with_v:
+                vcodes[d // 2], vscl[d // 2] = ecodes[d][:, 2 * P :], escl[d][:, 2 * P :]
 
         def regroup_v(h):
             if not 0 <= h < NH:
                 return
-            vg[h] = vgp.tile([P, DV, 4], BF16, name="vg", align_bytes=64)
+            if h < NH - 1:
+                gq[2 * h] = evp.tile([P, E_COLS + 4 * DV], BF16, name="gqv", align_bytes=64)
+                dst = gq[2 * h][:, E_COLS:]
+            else:
+                dst = v_last[:]
             nc.gpsimd.tensor_scalar(
-                out=vg[h][:],
+                out=dst.rearrange("p (c t) -> p c t", t=4),
                 in0=vr[h][:].rearrange("p t c -> p c t"),
                 scalar1=1.0,
                 scalar2=0.0,
                 op0=ALU.mult,
                 op1=ALU.add,
-            )
-
-        def quant_v(h):
-            if not 0 <= h < NH:
-                return
-            vcodes[h] = work.tile([P, DV], U32, name="vcodes", align_bytes=64)
-            vscl[h] = work.tile([P, DV], U8, name="vscl", align_bytes=64)
-            nc.vector.quantize_mx(
-                out=vcodes[h][:].bitcast(FP8X4),
-                scales=vscl[h][:],
-                in_=vg[h][:].rearrange("p c t -> p (c t)"),
             )
 
         def mx(d, jj):
@@ -244,8 +246,8 @@ def tile_attention_t_kernel(tc, q, k, v, pe_q, pe_k, mask, out):
                 out=ops[d][:, jj, :],
                 lhsT=ecodes[d][:, cols].bitcast(FP8X4),
                 lhsT_scale=escl[d][:, cols],
-                rhs=vcodes[h][:].bitcast(FP8X4),
-                rhs_scale=vscl[h][:],
+                rhs=vcodes[h].bitcast(FP8X4),
+                rhs_scale=vscl[h],
                 start=True,
                 stop=True,
             )
@@ -296,6 +298,7 @@ def tile_attention_t_kernel(tc, q, k, v, pe_q, pe_k, mask, out):
             else:
                 nc.vector.tensor_scalar(out=dst, in0=src, scalar1=-1.0, scalar2=BIG, op0=ALU.add, op1=ALU.mult)
 
+        v_last = const.tile([P, 4 * DV], BF16, name="v_last", align_bytes=64)
         ident_f = const.tile([P, P], F32, name="ident_f")
         ident_b = const.tile([P, P], BF16, name="ident_b")
         make_identity(nc, ident_f[:])
@@ -386,6 +389,7 @@ def tile_attention_t_kernel(tc, q, k, v, pe_q, pe_k, mask, out):
             recip(n - LAG_RC)
             quant_e(n - LAG_QE)
             if n % 2 == 0:
-                quant_v(n // 2 - 1)
                 regroup_v(n // 2)
+            if n == NSTEP:
+                quant_last_v()
             evac_d(n - LAG_EVD)

@@ -24,7 +24,8 @@ FLOPS = NH * (2 * 2 * L * L * D + 2 * L * L * DV)
 LAG_TS, LAG_EXP, LAG_T, LAG_EVC, LAG_QE, LAG_MX, LAG_EVD, LAG_RC = 1, 2, 2, 3, 4, 5, 5, 3
 TAIL_C = 4
 TAIL_D = 5
-MASK1_AT = 6
+N_PLAIN = 2
+MASK_AT = (2, 6)
 
 
 def tile_attention_t_kernel(tc, q, k, v, pe_q, pe_k, mask, out):
@@ -55,6 +56,13 @@ def tile_attention_t_kernel(tc, q, k, v, pe_q, pe_k, mask, out):
         def rows4(ap):
             return ap.rearrange("(a l) c -> a l c", l=4)
 
+        def load_q_half(l0):
+            nc.sync.dma_start(out=qq[0][:, l0 : l0 + 2, 0:D], in_=rows4(q[0, 0])[:, l0 : l0 + 2, :])
+            nc.sync.dma_start(out=qq[0][:, l0 : l0 + 2, D : 2 * D], in_=rows4(pe_q[0, 0])[:, l0 : l0 + 2, :])
+
+        def load_mask_half(l0):
+            nc.sync.dma_start(out=m_raw[0][:, l0 : l0 + 2, :], in_=rows4(mask[0])[:, l0 : l0 + 2, :])
+
         def load(h):
             b, hh = divmod(h, H)
             kk[h] = raw.tile([P, 4, 2 * D], BF16, name="kk")
@@ -62,10 +70,10 @@ def tile_attention_t_kernel(tc, q, k, v, pe_q, pe_k, mask, out):
             nc.sync.dma_start(out=kk[h][:, :, 0:D], in_=rows4(k[b, hh]))
             nc.sync.dma_start(out=kk[h][:, :, D : 2 * D], in_=rows4(pe_k[b, hh]))
             if h == 0:
-                for l0 in (0, 2):
-                    nc.sync.dma_start(out=qq[h][:, l0 : l0 + 2, 0:D], in_=rows4(q[b, hh])[:, l0 : l0 + 2, :])
-                    nc.sync.dma_start(out=qq[h][:, l0 : l0 + 2, D : 2 * D], in_=rows4(pe_q[b, hh])[:, l0 : l0 + 2, :])
-                    nc.sync.dma_start(out=m_raw[0][:, l0 : l0 + 2, :], in_=rows4(mask[0])[:, l0 : l0 + 2, :])
+                load_q_half(0)
+                load_mask_half(0)
+                load_q_half(2)
+                load_mask_half(2)
             else:
                 nc.sync.dma_start(out=qq[h][:, :, 0:D], in_=rows4(q[b, hh]))
                 nc.sync.dma_start(out=qq[h][:, :, D : 2 * D], in_=rows4(pe_q[b, hh]))
@@ -78,39 +86,38 @@ def tile_attention_t_kernel(tc, q, k, v, pe_q, pe_k, mask, out):
         def side(i):
             return (i % 2 == 0), (i + 2) // 2 if i % 2 == 0 else (i + 1) // 2
 
-        def a_transposes(i, blocks, borrowed=False):
+        def a_transposes(i, blocks, pool=None, tag=None):
             is_k, h = side(i)
             if not 0 <= h < NH:
                 return
             src = kk[h] if is_k else qq[h]
             src32 = src[:].rearrange("p l c -> p (l c)").bitcast(F32)
-            if blocks[0] == 0:
-                if borrowed:
-                    tps[i] = ps_c.tile([P, 4, P], F32, name="tps_start", tag="e_t")
-                else:
-                    tps[i] = ps_a.tile([P, 4, P], F32, name="tps")
             for l in blocks:
-                nc.tensor.transpose(tps[i][:, l, :], src32[:, l * P : (l + 1) * P], ident_f[:])
+                if pool is not None and l == blocks[0]:
+                    bank = pool.tile([P, 4, P], F32, name="tps_start", tag=tag)
+                elif l == 0:
+                    bank = ps_a.tile([P, 4, P], F32, name="tps")
+                else:
+                    bank = tps[(i, l - 1)]
+                tps[(i, l)] = bank
+                nc.tensor.transpose(bank[:, l, :], src32[:, l * P : (l + 1) * P], ident_f[:])
 
-        def evac_a(i, l0=0, l1=4):
+        def evac_a(i, l0=0, l1=4, copy=nc.scalar.copy):
             is_k, h = side(i)
             if not 0 <= h < NH:
                 return
+            bank = tps[(i, l0)]
             if is_k:
-                k_t[h] = tsb.tile([P, L], F32, name="k_t")
-                dst = k_t[h]
-            elif l0 == 0:
-                q_t[h] = tsb.tile([P, L], F32, name="q_t")
-                dst = q_t[h]
-            else:
-                dst = q_t[h]
-            if is_k:
-                nc.scalar.copy(
-                    out=dst[:].rearrange("p (u a e) -> p u a e", u=2, e=2),
-                    in_=tps[i][:].rearrange("p (u e) a -> p u a e", e=2),
+                if l0 == 0:
+                    k_t[h] = tsb.tile([P, L], F32, name="k_t")
+                copy(
+                    out=k_t[h][:, l0 * P : l1 * P].rearrange("p (u a e) -> p u a e", u=(l1 - l0) // 2, e=2),
+                    in_=bank[:, l0:l1, :].rearrange("p (u e) a -> p u a e", e=2),
                 )
             else:
-                nc.scalar.copy(out=dst[:, l0 * P : l1 * P], in_=tps[i][:, l0:l1, :].rearrange("p l a -> p (l a)"))
+                if l0 == 0:
+                    q_t[h] = tsb.tile([P, L], F32, name="q_t")
+                copy(out=q_t[h][:, l0 * P : l1 * P], in_=bank[:, l0:l1, :].rearrange("p l a -> p (l a)"))
 
         def score_mm(d, jj, e):
             if not live(d):
@@ -134,6 +141,9 @@ def tile_attention_t_kernel(tc, q, k, v, pe_q, pe_k, mask, out):
                 return
             b = d // (2 * H)
             j = 2 * (d % 2) + jj
+            if d < 2 * N_PLAIN:
+                nc.tensor.matmul(sps[(d, jj)][:], lhsT=ident_b[:], rhs=cap[b][:, j, :], start=False, stop=True)
+                return
             for t in blocks:
                 nc.tensor.matmul(
                     sps[(d, jj)][:, t * P : (t + 1) * P],
@@ -279,24 +289,32 @@ def tile_attention_t_kernel(tc, q, k, v, pe_q, pe_k, mask, out):
             j0 = 2 * (d % 2)
             nc.sync.dma_start(out=rows4(out[b, hh])[:, j0 : j0 + 2, :], in_=osb[d][:])
 
-        def mask_transposes(b, j):
-            m_t[(b, j)] = ps_s.tile([P, 4, P], BF16, name="m_t", tag="sps")
-            for t in range(4):
-                nc.tensor.transpose(m_t[(b, j)][:, t, :], m_perm[b][:, j, t * P : (t + 1) * P], ident_b[:])
+        def mask_transposes(b, j0, n_blocks):
+            if b == 0:
+                m_t[(b, j0)] = ps_d.tile([P, n_blocks, 4, P], BF16, name="m_t0", tag="ops")
+            else:
+                m_t[(b, j0)] = ps_s.tile([P, n_blocks, 4, P], BF16, name="m_t1", tag="sps")
+            for j in range(n_blocks):
+                for t in range(4):
+                    nc.tensor.transpose(m_t[(b, j0)][:, j, t, :], cap[b][:, j0 + j, t * P : (t + 1) * P], ident_b[:])
 
-        def mask_permute(b, j0, j1):
-            nc.vector.tensor_copy(
-                out=m_perm[b][:, j0:j1, :].bitcast(F32).rearrange("p j (u a) -> p j u a", u=2),
-                in_=m_raw[b][:, j0:j1, :].bitcast(F32).rearrange("p j (a u) -> p j u a", u=2),
+        def cap_build(b, j, engine):
+            engine.tensor_scalar(
+                out=cap[b][:, j, :].rearrange("p (u a e) -> p u a e", u=2, e=2),
+                in0=m_raw[b][:, j, :].rearrange("p (a u e) -> p u a e", u=2, e=2),
+                scalar1=-1.0,
+                scalar2=BIG,
+                op0=ALU.add,
+                op1=ALU.mult,
             )
 
-        def cap_build(b, j, on_scalar):
-            dst = cap_t[b][:, j, :, :].rearrange("p t q -> p (t q)")
-            src = m_t[(b, j)][:].rearrange("p t q -> p (t q)")
+        def cap_t_build(b, j0, j, on_scalar):
+            dst = cap_t[b][:, j0 + j, :, :].rearrange("p t q -> p (t q)")
+            src = m_t[(b, j0)][:, j, :, :].rearrange("p t q -> p (t q)")
             if on_scalar:
-                nc.scalar.activation(out=dst, in_=src, func=ACT.Copy, bias=-BIG, scale=BIG)
+                nc.scalar.copy(out=dst, in_=src)
             else:
-                nc.vector.tensor_scalar(out=dst, in0=src, scalar1=-1.0, scalar2=BIG, op0=ALU.add, op1=ALU.mult)
+                nc.vector.tensor_copy(out=dst, in_=src)
 
         v_last = const.tile([P, 4 * DV], BF16, name="v_last", align_bytes=64)
         ident_f = const.tile([P, P], F32, name="ident_f")
@@ -304,7 +322,7 @@ def tile_attention_t_kernel(tc, q, k, v, pe_q, pe_k, mask, out):
         make_identity(nc, ident_f[:])
         make_identity(nc, ident_b[:])
         m_raw = [const.tile([P, 4, L], BF16, name="m_raw%d" % b) for b in range(B)]
-        m_perm = [const.tile([P, 4, L], BF16, name="m_perm%d" % b) for b in range(B)]
+        cap = [const.tile([P, 4, L], BF16, name="cap%d" % b) for b in range(B)]
         cap_t = [const.tile([P, 4, 4, P], F32, name="cap_t%d" % b) for b in range(B)]
 
         warm = const.tile([P, 2 * P], BF16, name="warm")
@@ -321,40 +339,41 @@ def tile_attention_t_kernel(tc, q, k, v, pe_q, pe_k, mask, out):
         load(3)
         nc.sync.dma_start(out=m_raw[1][:], in_=rows4(mask[1]))
         load_v(2)
+        cap_build(0, 2, nc.gpsimd)
+        cap_build(0, 3, nc.gpsimd)
         regroup_v(0)
-        mask_permute(0, 0, 2)
 
-        a_transposes(-2, [0, 1, 2, 3])
+        a_transposes(-2, [0, 1, 2, 3], ps_c, "e_t")
         evac_a(-2)
-        a_transposes(-1, [0, 1], borrowed=True)
-        evac_a(-1, 0, 2)
-        mask_transposes(0, 0)
-        mask_transposes(0, 1)
-        cap_build(0, 0, False)
-        cap_build(0, 1, False)
-        for jj in range(2):
-            score_mm(0, jj, 0)
-            score_mm(0, jj, 1)
-            score_mask(0, jj, [0, 1, 2, 3])
-        scale_min(0, 0)
-        mask_permute(0, 2, 4)
-        exp(0, 0)
-        a_transposes(-1, [2, 3], borrowed=True)
+        a_transposes(-1, [0, 1], ps_c, "e_t")
+        evac_a(-1, 0, 2, nc.vector.tensor_copy)
+        cap_build(0, 0, nc.vector)
+        cap_build(0, 1, nc.vector)
+        score_mm(0, 0, 0)
+        score_mm(0, 0, 1)
+        score_mask(0, 0, [])
+        score_mm(0, 1, 0)
+        score_mm(0, 1, 1)
+        a_transposes(-1, [2, 3], ps_c, "e_t")
+        score_mask(0, 1, [])
         evac_a(-1, 2, 4)
-        a_transposes(0, [0, 1, 2, 3], borrowed=True)
-        evac_a(0)
-        mask_transposes(0, 2)
-        mask_transposes(0, 3)
+        scale_min(0, 0)
+        mask_transposes(0, 0, 2)
+        a_transposes(0, [0, 1, 2, 3])
         scale_min(0, 1)
-        cap_build(0, 2, False)
-        cap_build(0, 3, False)
-        exp(0, 1)
-        a_transposes(1, [0, 1, 2, 3])
+        exp(0, 0)
+        evac_a(0)
+        score_mm(1, 0, 0)
+        score_mm(1, 0, 1)
+        score_mask(1, 0, [])
+        a_transposes(1, [0, 1, 2, 3], ps_c, "e_t")
+        cap_t_build(0, 0, 0, False)
         evac_a(1)
-        for jj in range(2):
-            score_mm(1, jj, 0)
-            score_mm(1, jj, 1)
-            score_mask(1, jj, [0, 1, 2, 3])
+        score_mm(1, 1, 0)
+        score_mm(1, 1, 1)
+        score_mask(1, 1, [])
+        cap_t_build(0, 0, 1, False)
+        exp(0, 1)
 
         for n in range(2, NSTEP + LAG_EVD + 1):
             if n % 2 == 0 and n // 2 + 3 < NH:
@@ -366,10 +385,10 @@ def tile_attention_t_kernel(tc, q, k, v, pe_q, pe_k, mask, out):
             if n - LAG_EXP >= 1:
                 exp(n - LAG_EXP, 0)
                 exp(n - LAG_EXP, 1)
-            if n == MASK1_AT - 1:
-                mask_permute(1, 0, 4)
-            if MASK1_AT <= n < MASK1_AT + 4:
-                mask_transposes(1, n - MASK1_AT)
+            if MASK_AT[1] - 4 <= n < MASK_AT[1]:
+                cap_build(1, n - MASK_AT[1] + 4, nc.gpsimd)
+            if MASK_AT[1] <= n < MASK_AT[1] + 4:
+                mask_transposes(1, n - MASK_AT[1], 1)
             score_mm(n, 0, 0)
             a_transposes(n, [0, 1])
             score_mm(n, 0, 1)
@@ -384,8 +403,12 @@ def tile_attention_t_kernel(tc, q, k, v, pe_q, pe_k, mask, out):
             e_transposes(n - LAG_T, 0)
             e_transposes(n - LAG_T, 1)
             evac_c(n - LAG_EVC)
-            if MASK1_AT <= n < MASK1_AT + 4:
-                cap_build(1, n - MASK1_AT, n % 2 == 0)
+            if MASK_AT[1] <= n < MASK_AT[1] + 4:
+                cap_t_build(1, n - MASK_AT[1], 0, n % 2 == 0)
+            if n == 2:
+                mask_transposes(0, 2, 2)
+            if n in (3, 4):
+                cap_t_build(0, 2, n - 3, False)
             recip(n - LAG_RC)
             quant_e(n - LAG_QE)
             if n % 2 == 0:

@@ -15,16 +15,14 @@ B, H, L, D, DV = 2, 8, 512, 128, 256
 P = 128
 NH = B * H
 NSTEP = 2 * NH
-N_WARM = 7
 E_COLS = 2 * P * 4
 SCALE = D ** (-0.5)
 BIG = 1.0e30
 FLOPS = NH * (2 * 2 * L * L * D + 2 * L * L * DV)
 
 LAG_TS, LAG_EXP, LAG_T, LAG_EVC, LAG_QE, LAG_MX, LAG_EVD, LAG_RC = 1, 2, 2, 3, 4, 5, 5, 3
-TAIL_C = 4
-TAIL_D = 5
 N_PLAIN = 2
+V_MASK = [(0, 0), (0, 1)]
 MASK_AT = (2, 6)
 
 
@@ -38,7 +36,7 @@ def tile_attention_t_kernel(tc, q, k, v, pe_q, pe_k, mask, out):
         work = ctx.enter_context(tc.tile_pool(name="work", bufs=4))
         small = ctx.enter_context(tc.tile_pool(name="small", bufs=12))
         evp = ctx.enter_context(tc.tile_pool(name="evp", bufs=2))
-        outp = ctx.enter_context(tc.tile_pool(name="outp", bufs=4))
+        outp = ctx.enter_context(tc.tile_pool(name="outp", bufs=6))
         ps_s = ctx.enter_context(tc.psum_pool(name="ps_s", bufs=4))
         ps_a = ctx.enter_context(tc.psum_pool(name="ps_a", bufs=1))
         ps_c = ctx.enter_context(tc.psum_pool(name="ps_c", bufs=2))
@@ -49,6 +47,11 @@ def tile_attention_t_kernel(tc, q, k, v, pe_q, pe_k, mask, out):
         sps, tt, mn, ee, rsum, rs = {}, {}, {}, {}, {}, {}
         e_t, gq, ecodes, escl = {}, {}, {}, {}
         vcodes, vscl, ops, osb, m_t = {}, {}, {}, {}, {}
+
+        last = NSTEP - 1
+
+        def on_vector(d, jj):
+            return (d // 2, 2 * (d % 2) + jj) in V_MASK
 
         def live(d):
             return 0 <= d < NSTEP
@@ -133,7 +136,7 @@ def tile_attention_t_kernel(tc, q, k, v, pe_q, pe_k, mask, out):
                 lhsT=qb[:, j * P : (j + 1) * P, e],
                 rhs=kb[:, :, e],
                 start=(e == 0),
-                stop=False,
+                stop=(e == 1 and on_vector(d, jj)),
             )
 
         def score_mask(d, jj, blocks):
@@ -141,6 +144,8 @@ def tile_attention_t_kernel(tc, q, k, v, pe_q, pe_k, mask, out):
                 return
             b = d // (2 * H)
             j = 2 * (d % 2) + jj
+            if on_vector(d, jj):
+                return
             if d < 2 * N_PLAIN:
                 nc.tensor.matmul(sps[(d, jj)][:], lhsT=ident_b[:], rhs=cap[b][:, j, :], start=False, stop=True)
                 return
@@ -159,6 +164,17 @@ def tile_attention_t_kernel(tc, q, k, v, pe_q, pe_k, mask, out):
                 return
             tt[(d, jj)] = tts.tile([P, L], F32, name="tt")
             mn[(d, jj)] = small.tile([P, 1], F32, name="mn")
+            if on_vector(d, jj):
+                nc.vector.scalar_tensor_tensor(
+                    out=tt[(d, jj)][:],
+                    in0=sps[(d, jj)][:],
+                    scalar=-SCALE,
+                    in1=cap[d // (2 * H)][:, 2 * (d % 2) + jj, :],
+                    op0=ALU.mult,
+                    op1=ALU.subtract,
+                )
+                nc.vector.tensor_reduce(out=mn[(d, jj)][:], in_=tt[(d, jj)][:], axis=mybir.AxisListType.X, op=ALU.min)
+                return
             nc.vector.tensor_scalar(
                 out=tt[(d, jj)][:],
                 in0=sps[(d, jj)][:],
@@ -188,21 +204,23 @@ def tile_attention_t_kernel(tc, q, k, v, pe_q, pe_k, mask, out):
         def e_transposes(d, jj):
             if not live(d):
                 return
-            if jj == 0:
+            if jj == 0 and d < last:
                 e_t[d] = ps_c.tile([P, 2, 2, P], F32, name="e_t")
+            elif jj == 0:
+                e_t[d] = ps_s.tile([P, 2, 2, P], F32, name="e_t_last", tag="sps")
             words = ee[d][:].rearrange("p j c -> p (j c)").bitcast(F32)
             for u in range(2):
                 w0 = (2 * jj + u) * P
                 nc.tensor.transpose(e_t[d][:, jj, u, :], words[:, w0 : w0 + P], ident_f[:])
 
-        def evac_c(d):
+        def evac_c(d, on_vector=False):
             if not live(d):
                 return
             if d % 2 == 1 or d == NSTEP - 2:
                 gq[d] = work.tile([P, E_COLS], BF16, name="gq", align_bytes=64)
             src = e_t[d][:].rearrange("p j u q -> p j q u")
             dst = gq[d][:, 0:E_COLS].bitcast(F32).rearrange("p (j q u) -> p j q u", j=2, u=2)
-            if d >= NSTEP - TAIL_C and d % 2 == 1:
+            if on_vector:
                 nc.vector.tensor_copy(out=dst, in_=src)
             else:
                 nc.scalar.copy(out=dst, in_=src)
@@ -247,7 +265,7 @@ def tile_attention_t_kernel(tc, q, k, v, pe_q, pe_k, mask, out):
                 return
             h = d // 2
             if jj == 0:
-                if d >= NSTEP - TAIL_D:
+                if d >= last - 4:
                     ops[d] = ps_s.tile([P, 2, DV], F32, name="ops_tail", tag="sps")
                 else:
                     ops[d] = ps_d.tile([P, 2, DV], F32, name="ops")
@@ -268,12 +286,12 @@ def tile_attention_t_kernel(tc, q, k, v, pe_q, pe_k, mask, out):
             rs[d // 2] = small.tile([P, 4], F32, name="rs")
             nc.vector.reciprocal(out=rs[d // 2][:], in_=rsum[d // 2][:])
 
-        def evac_d(d):
+        def evac_d(d, on_scalar=False):
             if not live(d):
                 return
             osb[d] = outp.tile([P, 2, DV], F32, name="osb")
             r0 = 2 * (d % 2)
-            if d >= NSTEP - TAIL_D:
+            if on_scalar:
                 for jj in range(2):
                     nc.scalar.activation(
                         out=osb[d][:, jj, :], in_=ops[d][:, jj, :], func=ACT.Copy, scale=rs[d // 2][:, r0 + jj : r0 + jj + 1]
@@ -328,8 +346,12 @@ def tile_attention_t_kernel(tc, q, k, v, pe_q, pe_k, mask, out):
         warm = const.tile([P, 2 * P], BF16, name="warm")
         warm_ps = ps_s.tile([P, 2 * P], F32, name="warm_ps", tag="sps")
         nc.vector.memset(warm[:], 0.0)
-        for i in range(N_WARM):
-            nc.tensor.matmul(warm_ps[:], lhsT=warm[:, 0:P], rhs=warm[:], start=True, stop=True)
+
+        def warm_up(count):
+            for i in range(count):
+                nc.tensor.matmul(warm_ps[:], lhsT=warm[:, 0:P], rhs=warm[:], start=True, stop=True)
+
+        warm_up(10)
 
         load(0)
         load(1)
@@ -347,6 +369,7 @@ def tile_attention_t_kernel(tc, q, k, v, pe_q, pe_k, mask, out):
         evac_a(-2)
         a_transposes(-1, [0, 1], ps_c, "e_t")
         evac_a(-1, 0, 2, nc.vector.tensor_copy)
+        warm_up(3)
         cap_build(0, 0, nc.vector)
         cap_build(0, 1, nc.vector)
         score_mm(0, 0, 0)
@@ -361,8 +384,8 @@ def tile_attention_t_kernel(tc, q, k, v, pe_q, pe_k, mask, out):
         mask_transposes(0, 0, 2)
         a_transposes(0, [0, 1, 2, 3])
         scale_min(0, 1)
-        exp(0, 0)
         evac_a(0)
+        exp(0, 0)
         score_mm(1, 0, 0)
         score_mm(1, 0, 1)
         score_mask(1, 0, [])
@@ -375,7 +398,7 @@ def tile_attention_t_kernel(tc, q, k, v, pe_q, pe_k, mask, out):
         cap_t_build(0, 0, 1, False)
         exp(0, 1)
 
-        for n in range(2, NSTEP + LAG_EVD + 1):
+        for n in range(2, NSTEP):
             if n % 2 == 0 and n // 2 + 3 < NH:
                 load(n // 2 + 3)
             if n % 2 == 0 and n // 2 + 2 < NH:
@@ -393,11 +416,14 @@ def tile_attention_t_kernel(tc, q, k, v, pe_q, pe_k, mask, out):
             a_transposes(n, [0, 1])
             score_mm(n, 0, 1)
             a_transposes(n, [2, 3])
+            if n == last:
+                score_mask(n, 0, [0, 1, 2, 3])
             score_mm(n, 1, 0)
             mx(n - LAG_MX, 0)
             mx(n - LAG_MX, 1)
             score_mm(n, 1, 1)
-            score_mask(n, 0, [0, 1, 2, 3])
+            if n < last:
+                score_mask(n, 0, [0, 1, 2, 3])
             score_mask(n, 1, [0, 1, 2, 3])
             evac_a(n)
             e_transposes(n - LAG_T, 0)
@@ -409,10 +435,45 @@ def tile_attention_t_kernel(tc, q, k, v, pe_q, pe_k, mask, out):
                 mask_transposes(0, 2, 2)
             if n in (3, 4):
                 cap_t_build(0, 2, n - 3, False)
+            if n == last:
+                break
             recip(n - LAG_RC)
             quant_e(n - LAG_QE)
             if n % 2 == 0:
                 regroup_v(n // 2)
-            if n == NSTEP:
-                quant_last_v()
             evac_d(n - LAG_EVD)
+
+        quant_e(last - 4)
+        for jj in range(2):
+            scale_min(last, jj)
+        for jj in range(2):
+            exp(last - 1, jj)
+        for jj in range(2):
+            e_transposes(last - 1, jj)
+        for jj in range(2):
+            exp(last, jj)
+        mx(last - 4, 0)
+        mx(last - 4, 1)
+        evac_d(last - 5)
+        evac_d(last - 4)
+        for jj in range(2):
+            e_transposes(last, jj)
+        quant_e(last - 3)
+        quant_last_v()
+        evac_c(last - 2)
+        evac_c(last - 1)
+        evac_c(last)
+        recip(last - 2)
+        mx(last - 3, 0)
+        mx(last - 3, 1)
+        evac_d(last - 3, True)
+        quant_e(last - 2)
+        quant_e(last - 1)
+        quant_e(last)
+        recip(last)
+        for d in range(last - 2, last + 1):
+            mx(d, 0)
+            mx(d, 1)
+        evac_d(last - 2)
+        evac_d(last - 1, True)
+        evac_d(last)

from contextlib import ExitStack

import concourse.mybir as mybir
from concourse.masks import make_identity

F32 = mybir.dt.float32
BF16 = mybir.dt.bfloat16
U32 = mybir.dt.uint32
U8 = mybir.dt.uint8
FP8X4 = mybir.dt.float8_e4m3fn_x4
ALU = mybir.AluOpType
ACT = mybir.ActivationFunctionType

B, H, L, D, DV = 2, 8, 512, 128, 256
P = 128
NH = B * H
NSTEP = 2 * NH
E_COLS = 2 * P * 4
SCALE = D ** (-0.5)
BIG = 1.0e30
FLOPS = NH * (2 * 2 * L * L * D + 2 * L * L * DV)

LAG_TS, LAG_EXP, LAG_T, LAG_EVC, LAG_QE, LAG_MX, LAG_EVD, LAG_RC = 1, 2, 2, 3, 4, 5, 5, 3
N_PLAIN = 2
V_MASK = [(0, 0), (0, 1)]
MASK_AT = (2, 6)


def tile_attention_t_kernel(tc, q, k, v, pe_q, pe_k, mask, out):
    nc = tc.nc
    with ExitStack() as ctx:
        const = ctx.enter_context(tc.tile_pool(name="const", bufs=1))
        raw = ctx.enter_context(tc.tile_pool(name="raw", bufs=4))
        tsb = ctx.enter_context(tc.tile_pool(name="tsb", bufs=3))
        tts = ctx.enter_context(tc.tile_pool(name="tts", bufs=6))
        work = ctx.enter_context(tc.tile_pool(name="work", bufs=4))
        small = ctx.enter_context(tc.tile_pool(name="small", bufs=12))
        evp = ctx.enter_context(tc.tile_pool(name="evp", bufs=2))
        outp = ctx.enter_context(tc.tile_pool(name="outp", bufs=6))
        ps_s = ctx.enter_context(tc.psum_pool(name="ps_s", bufs=4))
        ps_a = ctx.enter_context(tc.psum_pool(name="ps_a", bufs=1))
        ps_c = ctx.enter_context(tc.psum_pool(name="ps_c", bufs=2))
        ps_d = ctx.enter_context(tc.psum_pool(name="ps_d", bufs=1))
        ctx.enter_context(tc.manual_schedule())

        qq, kk, vr, q_t, k_t, tps = {}, {}, {}, {}, {}, {}
        sps, tt, mn, ee, rsum, rs = {}, {}, {}, {}, {}, {}
        e_t, gq, ecodes, escl = {}, {}, {}, {}
        vcodes, vscl, ops, osb, m_t = {}, {}, {}, {}, {}

        last = NSTEP - 1

        def on_vector(d, jj):
            return (d // 2, 2 * (d % 2) + jj) in V_MASK

        def live(d):
            return 0 <= d < NSTEP

        def rows4(ap):
            return ap.rearrange("(a l) c -> a l c", l=4)

        def load_q_half(l0):
            nc.sync.dma_start(out=qq[0][:, l0 : l0 + 2, 0:D], in_=rows4(q[0, 0])[:, l0 : l0 + 2, :])
            nc.sync.dma_start(out=qq[0][:, l0 : l0 + 2, D : 2 * D], in_=rows4(pe_q[0, 0])[:, l0 : l0 + 2, :])

        def load_mask_half(l0):
            nc.sync.dma_start(out=m_raw[0][:, l0 : l0 + 2, :], in_=rows4(mask[0])[:, l0 : l0 + 2, :])

        def load(h):
            b, hh = divmod(h, H)
            kk[h] = raw.tile([P, 4, 2 * D], BF16, name="kk")
            qq[h] = raw.tile([P, 4, 2 * D], BF16, name="qq")
            nc.sync.dma_start(out=kk[h][:, :, 0:D], in_=rows4(k[b, hh]))
            nc.sync.dma_start(out=kk[h][:, :, D : 2 * D], in_=rows4(pe_k[b, hh]))
            if h == 0:
                load_q_half(0)
                load_mask_half(0)
                load_q_half(2)
                load_mask_half(2)
            else:
                nc.sync.dma_start(out=qq[h][:, :, 0:D], in_=rows4(q[b, hh]))
                nc.sync.dma_start(out=qq[h][:, :, D : 2 * D], in_=rows4(pe_q[b, hh]))

        def load_v(h):
            b, hh = divmod(h, H)
            vr[h] = raw.tile([P, 4, DV], BF16, name="vr")
            nc.sync.dma_start(out=vr[h][:], in_=rows4(v[b, hh]))

        def side(i):
            return (i % 2 == 0), (i + 2) // 2 if i % 2 == 0 else (i + 1) // 2

        def a_transposes(i, blocks, pool=None, tag=None):
            is_k, h = side(i)
            if not 0 <= h < NH:
                return
            src = kk[h] if is_k else qq[h]
            src32 = src[:].rearrange("p l c -> p (l c)").bitcast(F32)
            for l in blocks:
                if pool is not None and l == blocks[0]:
                    bank = pool.tile([P, 4, P], F32, name="tps_start", tag=tag)
                elif l == 0:
                    bank = ps_a.tile([P, 4, P], F32, name="tps")
                else:
                    bank = tps[(i, l - 1)]
                tps[(i, l)] = bank
                nc.tensor.transpose(bank[:, l, :], src32[:, l * P : (l + 1) * P], ident_f[:])

        def evac_a(i, l0=0, l1=4, copy=nc.scalar.copy):
            is_k, h = side(i)
            if not 0 <= h < NH:
                return
            bank = tps[(i, l0)]
            if is_k:
                if l0 == 0:
                    k_t[h] = tsb.tile([P, L], F32, name="k_t")
                copy(
                    out=k_t[h][:, l0 * P : l1 * P].rearrange("p (u a e) -> p u a e", u=(l1 - l0) // 2, e=2),
                    in_=bank[:, l0:l1, :].rearrange("p (u e) a -> p u a e", e=2),
                )
            else:
                if l0 == 0:
                    q_t[h] = tsb.tile([P, L], F32, name="q_t")
                copy(out=q_t[h][:, l0 * P : l1 * P], in_=bank[:, l0:l1, :].rearrange("p l a -> p (l a)"))

        def score_mm(d, jj, e):
            if not live(d):
                return
            h = d // 2
            j = 2 * (d % 2) + jj
            qb = q_t[h][:].bitcast(BF16).rearrange("p (c e) -> p c e", e=2)
            kb = k_t[h][:].bitcast(BF16).rearrange("p (c e) -> p c e", e=2)
            if e == 0:
                sps[(d, jj)] = ps_s.tile([P, L], F32, name="sps")
            nc.tensor.matmul(
                sps[(d, jj)][:],
                lhsT=qb[:, j * P : (j + 1) * P, e],
                rhs=kb[:, :, e],
                start=(e == 0),
                stop=(e == 1 and on_vector(d, jj)),
            )

        def score_mask(d, jj, blocks):
            if not live(d):
                return
            b = d // (2 * H)
            j = 2 * (d % 2) + jj
            if on_vector(d, jj):
                return
            if d < 2 * N_PLAIN:
                nc.tensor.matmul(sps[(d, jj)][:], lhsT=ident_b[:], rhs=cap[b][:, j, :], start=False, stop=True)
                return
            for t in blocks:
                nc.tensor.matmul(
                    sps[(d, jj)][:, t * P : (t + 1) * P],
                    lhsT=cap_t[b][:, j, t, :],
                    rhs=ident_f[:],
                    is_transpose=True,
                    start=False,
                    stop=(t == 3),
                )

        def scale_min(d, jj):
            if not live(d):
                return
            tt[(d, jj)] = tts.tile([P, L], F32, name="tt")
            mn[(d, jj)] = small.tile([P, 1], F32, name="mn")
            if on_vector(d, jj):
                nc.vector.scalar_tensor_tensor(
                    out=tt[(d, jj)][:],
                    in0=sps[(d, jj)][:],
                    scalar=-SCALE,
                    in1=cap[d // (2 * H)][:, 2 * (d % 2) + jj, :],
                    op0=ALU.mult,
                    op1=ALU.subtract,
                )
                nc.vector.tensor_reduce(out=mn[(d, jj)][:], in_=tt[(d, jj)][:], axis=mybir.AxisListType.X, op=ALU.min)
                return
            nc.vector.tensor_scalar(
                out=tt[(d, jj)][:],
                in0=sps[(d, jj)][:],
                scalar1=-SCALE,
                scalar2=None,
                op0=ALU.mult,
                op1=ALU.min,
                accum_out=mn[(d, jj)][:],
            )

        def exp(d, jj):
            if not live(d):
                return
            if jj == 0:
                ee[d] = work.tile([P, 2, L], BF16, name="ee")
                if d % 2 == 0:
                    rsum[d // 2] = small.tile([P, 4], F32, name="rsum")
            nc.scalar.activation(
                out=ee[d][:, jj, :],
                in_=tt[(d, jj)][:],
                func=ACT.Exp,
                bias=mn[(d, jj)][:],
                scale=-1.0,
                accum_out=rsum[d // 2][:, 2 * (d % 2) + jj : 2 * (d % 2) + jj + 1],
            )

        def e_transposes(d, jj):
            if not live(d):
                return
            if jj == 0 and d < last:
                e_t[d] = ps_c.tile([P, 2, 2, P], F32, name="e_t")
            elif jj == 0:
                e_t[d] = ps_s.tile([P, 2, 2, P], F32, name="e_t_last", tag="sps")
            words = ee[d][:].rearrange("p j c -> p (j c)").bitcast(F32)
            for u in range(2):
                w0 = (2 * jj + u) * P
                nc.tensor.transpose(e_t[d][:, jj, u, :], words[:, w0 : w0 + P], ident_f[:])

        def evac_c(d, on_vector=False):
            if not live(d):
                return
            if d % 2 == 1 or d == NSTEP - 2:
                gq[d] = work.tile([P, E_COLS], BF16, name="gq", align_bytes=64)
            src = e_t[d][:].rearrange("p j u q -> p j q u")
            dst = gq[d][:, 0:E_COLS].bitcast(F32).rearrange("p (j q u) -> p j q u", j=2, u=2)
            if on_vector:
                nc.vector.tensor_copy(out=dst, in_=src)
            else:
                nc.scalar.copy(out=dst, in_=src)

        def quantize(values, width):
            codes = work.tile([P, width], U32, name="codes%d" % width, align_bytes=64)
            scales = work.tile([P, width], U8, name="scales%d" % width, align_bytes=64)
            nc.vector.quantize_mx(out=codes[:].bitcast(FP8X4), scales=scales[:], in_=values)
            return codes, scales

        def quant_last_v():
            codes, scales = quantize(v_last[:], DV)
            vcodes[NH - 1], vscl[NH - 1] = codes[:], scales[:]

        def quant_e(d):
            if not live(d):
                return
            with_v = d % 2 == 0 and d < NSTEP - 2
            ecodes[d], escl[d] = quantize(gq[d][:], 2 * P + (DV if with_v else 0))
            if with_v:
                vcodes[d // 2], vscl[d // 2] = ecodes[d][:, 2 * P :], escl[d][:, 2 * P :]

        def regroup_v(h):
            if not 0 <= h < NH:
                return
            if h < NH - 1:
                gq[2 * h] = evp.tile([P, E_COLS + 4 * DV], BF16, name="gqv", align_bytes=64)
                dst = gq[2 * h][:, E_COLS:]
            else:
                dst = v_last[:]
            nc.gpsimd.tensor_scalar(
                out=dst.rearrange("p (c t) -> p c t", t=4),
                in0=vr[h][:].rearrange("p t c -> p c t"),
                scalar1=1.0,
                scalar2=0.0,
                op0=ALU.mult,
                op1=ALU.add,
            )

        def mx(d, jj):
            if not live(d):
                return
            h = d // 2
            if jj == 0:
                if d >= last - 4:
                    ops[d] = ps_s.tile([P, 2, DV], F32, name="ops_tail", tag="sps")
                else:
                    ops[d] = ps_d.tile([P, 2, DV], F32, name="ops")
            cols = slice(jj * P, (jj + 1) * P)
            nc.tensor.matmul_mx(
                out=ops[d][:, jj, :],
                lhsT=ecodes[d][:, cols].bitcast(FP8X4),
                lhsT_scale=escl[d][:, cols],
                rhs=vcodes[h].bitcast(FP8X4),
                rhs_scale=vscl[h],
                start=True,
                stop=True,
            )

        def recip(d):
            if not live(d) or d % 2 == 0:
                return
            rs[d // 2] = small.tile([P, 4], F32, name="rs")
            nc.vector.reciprocal(out=rs[d // 2][:], in_=rsum[d // 2][:])

        def evac_d(d, on_scalar=False):
            if not live(d):
                return
            osb[d] = outp.tile([P, 2, DV], F32, name="osb")
            r0 = 2 * (d % 2)
            if on_scalar:
                for jj in range(2):
                    nc.scalar.activation(
                        out=osb[d][:, jj, :], in_=ops[d][:, jj, :], func=ACT.Copy, scale=rs[d // 2][:, r0 + jj : r0 + jj + 1]
                    )
            else:
                nc.vector.tensor_tensor(
                    out=osb[d][:],
                    in0=ops[d][:],
                    in1=rs[d // 2][:, r0 : r0 + 2].unsqueeze(2).to_broadcast([P, 2, DV]),
                    op=ALU.mult,
                )
            b, hh = divmod(d // 2, H)
            j0 = 2 * (d % 2)
            nc.sync.dma_start(out=rows4(out[b, hh])[:, j0 : j0 + 2, :], in_=osb[d][:])

        def mask_transposes(b, j0, n_blocks):
            if b == 0:
                m_t[(b, j0)] = ps_d.tile([P, n_blocks, 4, P], BF16, name="m_t0", tag="ops")
            else:
                m_t[(b, j0)] = ps_s.tile([P, n_blocks, 4, P], BF16, name="m_t1", tag="sps")
            for j in range(n_blocks):
                for t in range(4):
                    nc.tensor.transpose(m_t[(b, j0)][:, j, t, :], cap[b][:, j0 + j, t * P : (t + 1) * P], ident_b[:])

        def cap_build(b, j, engine):
            engine.tensor_scalar(
                out=cap[b][:, j, :].rearrange("p (u a e) -> p u a e", u=2, e=2),
                in0=m_raw[b][:, j, :].rearrange("p (a u e) -> p u a e", u=2, e=2),
                scalar1=-1.0,
                scalar2=BIG,
                op0=ALU.add,
                op1=ALU.mult,
            )

        def cap_t_build(b, j0, j, on_scalar):
            dst = cap_t[b][:, j0 + j, :, :].rearrange("p t q -> p (t q)")
            src = m_t[(b, j0)][:, j, :, :].rearrange("p t q -> p (t q)")
            if on_scalar:
                nc.scalar.copy(out=dst, in_=src)
            else:
                nc.vector.tensor_copy(out=dst, in_=src)

        v_last = const.tile([P, 4 * DV], BF16, name="v_last", align_bytes=64)
        ident_f = const.tile([P, P], F32, name="ident_f")
        ident_b = const.tile([P, P], BF16, name="ident_b")
        make_identity(nc, ident_f[:])
        make_identity(nc, ident_b[:])
        m_raw = [const.tile([P, 4, L], BF16, name="m_raw%d" % b) for b in range(B)]
        cap = [const.tile([P, 4, L], BF16, name="cap%d" % b) for b in range(B)]
        cap_t = [const.tile([P, 4, 4, P], F32, name="cap_t%d" % b) for b in range(B)]

        warm = const.tile([P, 2 * P], BF16, name="warm")
        warm_ps = ps_s.tile([P, 2 * P], F32, name="warm_ps", tag="sps")
        nc.vector.memset(warm[:], 0.0)

        def warm_up(count):
            for i in range(count):
                nc.tensor.matmul(warm_ps[:], lhsT=warm[:, 0:P], rhs=warm[:], start=True, stop=True)

        warm_up(10)

        load(0)
        load(1)
        load_v(0)
        load(2)
        load_v(1)
        load(3)
        nc.sync.dma_start(out=m_raw[1][:], in_=rows4(mask[1]))
        load_v(2)
        cap_build(0, 2, nc.gpsimd)
        cap_build(0, 3, nc.gpsimd)
        regroup_v(0)

        a_transposes(-2, [0, 1, 2, 3], ps_c, "e_t")
        evac_a(-2)
        a_transposes(-1, [0, 1], ps_c, "e_t")
        evac_a(-1, 0, 2, nc.vector.tensor_copy)
        warm_up(3)
        cap_build(0, 0, nc.vector)
        cap_build(0, 1, nc.vector)
        score_mm(0, 0, 0)
        score_mm(0, 0, 1)
        score_mask(0, 0, [])
        score_mm(0, 1, 0)
        score_mm(0, 1, 1)
        a_transposes(-1, [2, 3], ps_c, "e_t")
        score_mask(0, 1, [])
        evac_a(-1, 2, 4)
        scale_min(0, 0)
        mask_transposes(0, 0, 2)
        a_transposes(0, [0, 1, 2, 3])
        scale_min(0, 1)
        evac_a(0)
        exp(0, 0)
        score_mm(1, 0, 0)
        score_mm(1, 0, 1)
        score_mask(1, 0, [])
        a_transposes(1, [0, 1, 2, 3], ps_c, "e_t")
        cap_t_build(0, 0, 0, False)
        evac_a(1)
        score_mm(1, 1, 0)
        score_mm(1, 1, 1)
        score_mask(1, 1, [])
        cap_t_build(0, 0, 1, False)
        exp(0, 1)

        for n in range(2, NSTEP):
            if n % 2 == 0 and n // 2 + 3 < NH:
                load(n // 2 + 3)
            if n % 2 == 0 and n // 2 + 2 < NH:
                load_v(n // 2 + 2)
            scale_min(n - LAG_TS, 0)
            scale_min(n - LAG_TS, 1)
            if n - LAG_EXP >= 1:
                exp(n - LAG_EXP, 0)
                exp(n - LAG_EXP, 1)
            if MASK_AT[1] - 4 <= n < MASK_AT[1]:
                cap_build(1, n - MASK_AT[1] + 4, nc.gpsimd)
            if MASK_AT[1] <= n < MASK_AT[1] + 4:
                mask_transposes(1, n - MASK_AT[1], 1)
            score_mm(n, 0, 0)
            a_transposes(n, [0, 1])
            score_mm(n, 0, 1)
            a_transposes(n, [2, 3])
            if n == last:
                score_mask(n, 0, [0, 1, 2, 3])
            score_mm(n, 1, 0)
            mx(n - LAG_MX, 0)
            mx(n - LAG_MX, 1)
            score_mm(n, 1, 1)
            if n < last:
                score_mask(n, 0, [0, 1, 2, 3])
            score_mask(n, 1, [0, 1, 2, 3])
            evac_a(n)
            e_transposes(n - LAG_T, 0)
            e_transposes(n - LAG_T, 1)
            evac_c(n - LAG_EVC)
            if MASK_AT[1] <= n < MASK_AT[1] + 4:
                cap_t_build(1, n - MASK_AT[1], 0, n % 2 == 0)
            if n == 2:
                mask_transposes(0, 2, 2)
            if n in (3, 4):
                cap_t_build(0, 2, n - 3, False)
            if n == last:
                break
            recip(n - LAG_RC)
            quant_e(n - LAG_QE)
            if n % 2 == 0:
                regroup_v(n // 2)
            evac_d(n - LAG_EVD)

        quant_e(last - 4)
        for jj in range(2):
            scale_min(last, jj)
        for jj in range(2):
            exp(last - 1, jj)
        for jj in range(2):
            e_transposes(last - 1, jj)
        for jj in range(2):
            exp(last, jj)
        mx(last - 4, 0)
        mx(last - 4, 1)
        evac_d(last - 5)
        evac_d(last - 4)
        for jj in range(2):
            e_transposes(last, jj)
        quant_e(last - 3)
        quant_last_v()
        evac_c(last - 2)
        evac_c(last - 1)
        evac_c(last)
        recip(last - 2)
        mx(last - 3, 0)
        mx(last - 3, 1)
        evac_d(last - 3, True)
        quant_e(last - 2)
        quant_e(last - 1)
        quant_e(last)
        recip(last)
        for d in range(last - 2, last + 1):
            mx(d, 0)
            mx(d, 1)
        evac_d(last - 2)
        evac_d(last - 1, True)
        evac_d(last)
